import numpy as np
import ml_dtypes


def mxq(x, axis, fmt="e4m3"):
    dtype, down = {"e4m3": (ml_dtypes.float8_e4m3fn, 7), "e5m2": (ml_dtypes.float8_e5m2, 14)}[fmt]
    v = np.moveaxis(np.asarray(x, np.float32).astype(ml_dtypes.bfloat16).astype(np.float64), axis, -1)
    blocks = v.reshape(v.shape[:-1] + (-1, 32))
    amax = np.abs(blocks).max(-1, keepdims=True)
    byte = np.maximum(np.where(amax > 0, np.frexp(amax)[1] - 1 + 127, 0) - down, 1)
    scale = np.exp2(byte - 127.0)
    codes = (blocks / scale).astype(np.float32).astype(dtype).astype(np.float64)
    return np.moveaxis((codes * scale).reshape(v.shape), -1, axis)


WIDE = False


def mx_kscale(k):
    if not WIDE:
        return np.ones(k)
    levels = np.array([10, -10, 5, -5, 0])
    if k % 512:
        return np.exp2(np.random.permutation(np.resize(levels, k // 32))).repeat(32)
    a = np.empty((k // 512, 16))
    for p in range(k // 512):
        a[p, :8] = np.random.permutation(np.resize(levels, 8))
        for g in range(8):
            far = levels[np.abs(levels - a[p, g]) >= 10]
            a[p, g + 8] = far[np.random.randint(len(far))]
    return np.exp2(a.ravel()).repeat(32)


BF16 = ml_dtypes.bfloat16


def bf(x):
    return np.asarray(x, np.float32).astype(BF16)


def f64(x):
    return np.asarray(x).astype(np.float64)


E2M1 = np.array([0.0, 0.5, 1.0, 1.5, 2.0, 3.0, 4.0, 6.0, -0.0, -0.5, -1.0, -1.5, -2.0, -3.0, -4.0, -6.0])


def pack_weight(w, fmt):
    k, n = w.shape
    w = f64(bf(w)).reshape(k // 32, 32, n)
    amax = np.abs(w).max(1)
    if fmt == "e4m3":
        byte = np.frexp(amax)[1] - 1 + 127 - 7
    else:
        mant, ex = np.frexp(amax / 6.0)
        byte = np.where(mant > 0.5, ex, ex - 1) + 127
    byte = np.clip(np.where(amax > 0, byte, 1), 1, 254)
    scaled = (w * np.exp2(127.0 - byte)[:, None, :]).reshape(k, n).astype(np.float32)
    by_word = np.ascontiguousarray(scaled.reshape(k // 512, 128, 4, n).transpose(0, 1, 3, 2))
    if fmt == "e4m3":
        words = by_word.astype(ml_dtypes.float8_e4m3fn).view(np.uint8)
    else:
        c = by_word.astype(ml_dtypes.float4_e2m1fn).view(np.uint8) & 0xF
        words = c[..., 0::2] | (c[..., 1::2] << 4)
    return np.ascontiguousarray(words), np.ascontiguousarray(byte.astype(np.uint8).reshape(k // 512, 16, n))


def unpack_weight(words, scales, fmt):
    g, p, n, _ = words.shape
    if fmt == "e4m3":
        vals = np.ascontiguousarray(words).view(ml_dtypes.float8_e4m3fn).astype(np.float64)
    else:
        nib = np.empty((g, p, n, 4), np.uint8)
        nib[..., 0::2] = words & 0xF
        nib[..., 1::2] = words >> 4
        vals = E2M1[nib]
    vals = vals * np.repeat(np.exp2(scales.astype(np.float64) - 127.0), 8, axis=1)[..., None]
    return vals.transpose(0, 1, 3, 2).reshape(g * 512, n)
def pack4(w):
    words, scales = pack_weight(w, "e2m1")
    return words.reshape(words.shape[0], 128, -1), scales


def unpack4(words, scales):
    return unpack_weight(words.reshape(words.shape[0], 128, -1, 2), scales, "e2m1")


B, A, C, D, K0, K1, K2 = 2, 128, 64, 512, 512, 128, 256
D2 = D + D
NEG_SLOPE = 0.01


def leaky(v):
    return np.where(v >= 0, v, NEG_SLOPE * v)


def draw0():
    s, t = mx_kscale(D), mx_kscale(K0)
    ss = np.concatenate([s, s])
    sent_a = bf(np.random.standard_normal((B, A, D)) * s)
    sent_b = bf(np.random.standard_normal((B, C, D)) * s)
    W1_words, W1_scales = pack4(np.random.standard_normal((D2, K0)) / np.sqrt(D2) / ss[:, None] * t)
    b1 = bf((np.random.standard_normal(K0) * 0.5 - 0.5) * t)
    W2_words, W2_scales = pack4(np.random.standard_normal((K0, K1)) * 2.0 / np.sqrt(K0) / t[:, None])
    b2 = bf(np.random.standard_normal(K1) * 0.5 - 0.5)
    return {"sent_a": sent_a,
            "sent_b": sent_b,
            "W1_words": W1_words,
            "W1_scales": W1_scales,
            "b1": b1,
            "W2_words": W2_words,
            "W2_scales": W2_scales,
            "b2": b2}


def core(sent_a, sent_b, W1_words, W1_scales, b1, W2_words, W2_scales, b2):
    w1 = unpack4(W1_words, W1_scales)
    a_part = mxq(f64(sent_a), 2, "e4m3") @ w1[:D]
    b_part = mxq(f64(sent_b), 2, "e4m3") @ w1[D:]
    h = leaky(a_part[:, :, None, :] + b_part[:, None, :, :] + f64(b1))
    return leaky((mxq(h, 3, "e4m3") @ unpack4(W2_words, W2_scales)) + f64(b2))


def e4m3fn_bytes(y):
    return np.clip(np.asarray(y, np.float64), -448.0, 448.0).astype(np.float32).astype(ml_dtypes.float8_e4m3fn).view(np.uint8)


def e4m3fn_values(b):
    return np.asarray(b, np.uint8).view(ml_dtypes.float8_e4m3fn).astype(np.float64)


def setup_inputs():
    d = draw0()
    x0 = np.asarray(d['sent_a']).astype(np.float64)
    s = (np.max(np.abs(x0), axis=(0, 1), keepdims=True) / 448.0).astype(np.float32)
    out = {}
    for k, v in d.items():
        if k == 'sent_a':
            out['sent_a_bytes'] = e4m3fn_bytes(x0 / s.astype(np.float64))
            out['sent_a_scale'] = s
        else:
            out[k] = v
    return out


def reference(sent_a_bytes, sent_a_scale, sent_b, W1_words, W1_scales, b1, W2_words, W2_scales, b2):
    return core(e4m3fn_values(sent_a_bytes) * sent_a_scale.astype(np.float64), sent_b, W1_words, W1_scales, b1, W2_words, W2_scales, b2)

@@ -1,0 +1,391 @@
+from contextlib import ExitStack
+
+import concourse.mybir as mybir
+from concourse.masks import make_identity
+
+F32 = mybir.dt.float32
+BF16 = mybir.dt.bfloat16
+I32 = mybir.dt.int32
+U32 = mybir.dt.uint32
+U8 = mybir.dt.uint8
+FP8 = mybir.dt.float8_e4m3fn
+FP8X4 = mybir.dt.float8_e4m3fn_x4
+FP4X4 = mybir.dt.float4_e2m1fn_x4
+ALU = mybir.AluOpType
+COPY = mybir.ActivationFunctionType.Copy
+
+P = 128
+NB, NI, NJ, D, K0, K1 = 2, 128, 64, 512, 512, 128
+FLOPS = 2 * (NB * (NI + NJ) * D * K0 + NB * NI * NJ * K0 * K1)
+SLOPE = 0.01
+R = 8
+W = 8
+Z = 16
+QUAD = 4
+LATE = 2
+
+
+def tile_matchmatrix_pa_t_w4_kernel(
+    tc, sent_a_bytes, sent_a_scale, sent_b, w1_words, w1_scales, b1, w2_words, w2_scales, b2, out
+):
+    nc = tc.nc
+    with ExitStack() as ctx:
+        keep = ctx.enter_context(tc.tile_pool(name="keep", bufs=1))
+        work = ctx.enter_context(tc.tile_pool(name="work", bufs=4))
+        xps = ctx.enter_context(tc.psum_pool(name="xps", bufs=6))
+        yps = ctx.enter_context(tc.psum_pool(name="yps", bufs=2))
+        ctx.enter_context(tc.manual_schedule())
+
+        b_raw = keep.tile([P, D], BF16, align_bytes=64)
+        nc.sync.dma_start(out=b_raw[:], in_=sent_b.rearrange("n j k -> (n j) k"))
+        a_scale = keep.tile([P, 4], F32)
+        nc.scalar.dma_start(out=a_scale[:], in_=sent_a_scale.rearrange("x y (p t) -> p (x y t)", t=4))
+        a_bytes = keep.tile([P, NB, D], U8, align_bytes=64)
+        nc.sync.dma_start(out=a_bytes[:], in_=sent_a_bytes.rearrange("n i k -> i n k"))
+        b1_all = keep.tile([P, K0], BF16)
+        nc.scalar.dma_start(out=b1_all[:], in_=b1.partition_broadcast(P))
+        w1 = keep.tile([P, 2, 2 * K0], U8, align_bytes=64)
+        w1_sc = keep.tile([P, 2, K0], U8, align_bytes=64)
+        w2 = keep.tile([P, 2 * K1], U8, align_bytes=64)
+        w2_sc = keep.tile([P, K1], U8, align_bytes=64)
+        b_scales = keep.tile([P, P], U8, align_bytes=64)
+        probe = keep.tile([P, 1], F32)
+        idle = keep.tile([P, 4 * P], BF16)
+        nc.vector.memset(idle[:], 0.0)
+        nc.vector.memset(w1_sc[:].rearrange("p g n -> p (g n)").bitcast(I32), 0)
+        nc.vector.memset(probe[:], 0.0)
+        nc.vector.memset(b_scales[:].bitcast(I32), 0)
+        nc.vector.memset(w2_sc[:].bitcast(I32), 0)
+        for g in (1, 0):
+            nc.sync.dma_start(out=w1[:, g, :].bitcast(I32), in_=w1_words[g].bitcast(I32))
+        for q in range(4):
+            nc.sync.dma_start(
+                out=w1_sc[32 * q : 32 * q + 4, :, :].bitcast(I32),
+                in_=w1_scales[:, 4 * q : 4 * q + 4, :].rearrange("g q n -> q g n").bitcast(I32),
+            )
+        warm = keep.tile([P, 1], F32)
+        nc.scalar.activation(out=warm[:], in_=probe[:], func=COPY, scale=SLOPE)
+        b2_all = keep.tile([P, K1], BF16)
+        nc.sync.dma_start(out=b2_all[:], in_=b2.partition_broadcast(P))
+        nc.sync.dma_start(out=w2[:].bitcast(I32), in_=w2_words[0].bitcast(I32))
+        for q in range(4):
+            nc.sync.dma_start(
+                out=w2_sc[32 * q : 32 * q + 4, :].bitcast(I32),
+                in_=w2_scales[0, 4 * q : 4 * q + 4, :].bitcast(I32),
+            )
+
+        ident = keep.tile([P, P], F32)
+        make_identity(nc, ident[:])
+        shifts = keep.tile([P, 2 * W, Z], F32)
+        for half in range(2):
+            nc.vector.tensor_copy(
+                out=shifts[:, half * W : (half + 1) * W, :], in_=ident[:].rearrange("q (z w) -> q w z", w=W)
+            )
+
+        def turn(raw):
+            words = raw.bitcast(F32)
+            xt = xps.tile([P, 2, P], F32, name="xt", tag="x")
+            for u in range(2):
+                nc.tensor.transpose(xt[:, u, :], words[:, u : 2 * P : 2], ident[:])
+            return xt
+
+        def widen(n):
+            a_raw = keep.tile([P, D], BF16, align_bytes=64, name=f"a_raw{n}")
+            nc.scalar.copy(out=a_raw[:], in_=a_bytes[:, n, :].bitcast(FP8))
+            return a_raw
+
+        b_grouped = keep.tile([P, P, 4], BF16, align_bytes=64)
+        b_codes = keep.tile([P, P], U32, align_bytes=64)
+        rep_codes = keep.tile([P, NB, R, Z, W], U32, align_bytes=64)
+        rep_scales = keep.tile([P, NB, R, Z, W], U8, align_bytes=64)
+
+        def repeat_b(n, r0, r1):
+            cols = slice(n * NJ + r0 * W, n * NJ + r1 * W)
+            nr = r1 - r0
+            nc.vector.tensor_copy(
+                out=rep_codes[:, n, r0:r1].rearrange("p r z w -> p (r z w)").bitcast(I32).rearrange("p (r z w) -> p r z w", r=nr, z=Z),
+                in_=b_codes[:, cols].bitcast(I32).rearrange("p (r w) -> p r w", r=nr).unsqueeze(2).to_broadcast([P, nr, Z, W]),
+            )
+            nc.vector.tensor_copy(
+                out=rep_scales[:, n, r0:r1].rearrange("p r z w -> p (r z w)").bitcast(I32).rearrange("p (r z w) -> p r z w", r=nr, z=Z),
+                in_=b_scales[:, cols]
+                .bitcast(I32)
+                .rearrange("p (r w) -> p r w", r=nr)
+                .unsqueeze(2)
+                .to_broadcast([P, nr, Z, W // 4]),
+            )
+
+        def group_a(n, xt):
+            a_mixed = keep.tile([P, P, 4], BF16, align_bytes=64, name=f"a_mixed{n}")
+            nc.scalar.copy(
+                out=a_mixed[:].rearrange("p c t -> p (c t)").bitcast(F32).rearrange("p (c u) -> p c u", u=2),
+                in_=xt[:].rearrange("p u c -> p c u"),
+            )
+            return a_mixed
+
+        def scale_a(n, a_mixed):
+            a_grouped = keep.tile([P, P, 4], BF16, align_bytes=64, name=f"a_grouped{n}")
+            nc.vector.tensor_tensor(
+                out=a_grouped[:], in0=a_mixed[:], in1=a_scale[:].unsqueeze(1).to_broadcast([P, P, 4]), op=ALU.mult
+            )
+            return a_grouped
+
+        def quantize_a(n, a_grouped):
+            a_codes = keep.tile([P, P], U32, align_bytes=64, name=f"a_codes{n}")
+            a_scales = keep.tile([P, P], U8, align_bytes=64, name=f"a_scales{n}")
+            nc.vector.quantize_mx(
+                out=a_codes[:].bitcast(FP8X4), scales=a_scales[:], in_=a_grouped[:].rearrange("p c t -> p (c t)")
+            )
+            return a_codes, a_scales
+
+        a_part = keep.tile([P, NB, 4, P], F32)
+        b_part = keep.tile([P, NB, R, 4, P], F32)
+
+        def a_layer(n, a_codes, a_scales):
+            pa = xps.tile([P, K0], F32, name="pa", tag="x")
+            nc.tensor.matmul_mx(
+                out=pa[:],
+                lhsT=a_codes[:].bitcast(FP8X4),
+                lhsT_scale=a_scales[:],
+                rhs=w1[:, 0, :].bitcast(FP4X4),
+                rhs_scale=w1_sc[:, 0, :],
+                start=True,
+                stop=True,
+            )
+            nc.vector.tensor_tensor(
+                out=a_part[:, n],
+                in0=pa[:].rearrange("i (m t) -> i t m", t=4),
+                in1=b1_all[:].rearrange("i (m t) -> i t m", t=4),
+                op=ALU.add,
+            )
+
+        def b_layer(n, r, scalar):
+            pb = xps.tile([P, K0], F32, name="pb", tag="x")
+            nc.tensor.matmul_mx(
+                out=pb[:],
+                lhsT=rep_codes[:, n, r].rearrange("p z w -> p (z w)").bitcast(FP8X4),
+                lhsT_scale=rep_scales[:, n, r].rearrange("p z w -> p (z w)"),
+                rhs=w1[:, 1, :].bitcast(FP4X4),
+                rhs_scale=w1_sc[:, 1, :],
+                start=True,
+                stop=True,
+            )
+            dst = b_part[:, n, r]
+            view = pb[:].rearrange("q (m t) -> q t m", t=4)
+            if scalar:
+                nc.scalar.copy(out=dst, in_=view)
+            else:
+                nc.vector.tensor_copy(out=dst, in_=view)
+
+        def park_b():
+            pb = xps.tile([P, K0], F32, name="pb", tag="x")
+            nc.tensor.matmul_mx(
+                out=pb[:],
+                lhsT=b_codes[:].bitcast(FP8X4),
+                lhsT_scale=b_scales[:],
+                rhs=w1[:, 1, :].bitcast(FP4X4),
+                rhs_scale=w1_sc[:, 1, :],
+                start=True,
+                stop=True,
+            )
+            b_rows = keep.tile([P, 4, P], F32)
+            nc.scalar.copy(out=b_rows[:], in_=pb[:].rearrange("q (m t) -> q t m", t=4))
+            park = out[1, 120:124].rearrange("i j k -> (i j k)")
+            nc.sync.dma_start(
+                out=park.rearrange("(j c) -> j c", c=K0), in_=b_rows[NJ:, :, :].rearrange("j t m -> j (t m)")
+            )
+            rows = park.rearrange("(r w c) -> w r c", r=R, w=W)
+            for w in range(W):
+                nc.sync.dma_start(
+                    out=b_part[w::W, 1].rearrange("q r t m -> q r (t m)"), in_=rows[w].partition_broadcast(Z)
+                )
+
+        spin = yps.tile([P, 4 * P], F32, name="spin", tag="y")
+
+        def turn_over(times):
+            for i in range(times):
+                nc.tensor.matmul(spin[:], lhsT=idle[:, :P], rhs=idle[:], start=True, stop=True)
+
+        def group_b(n):
+            half = slice(n * NJ, (n + 1) * NJ)
+            nc.vector.tensor_copy(
+                out=b_grouped[:, half, :]
+                .rearrange("p c t -> p (c t)")
+                .bitcast(F32)
+                .rearrange("p (r w u) -> p r w u", r=R, w=W),
+                in_=xt_b[:, :, half].rearrange("p u (w r) -> p r w u", r=R),
+            )
+
+        def quantize_b(n):
+            half = slice(n * NJ, (n + 1) * NJ)
+            nc.vector.quantize_mx(
+                out=b_codes[:, half].bitcast(FP8X4),
+                scales=b_scales[:, half],
+                in_=b_grouped[:, half, :].rearrange("p c t -> p (c t)"),
+            )
+
+        turn_over(3)
+        xt_b = turn(b_raw[:])
+        turn_over(2)
+        a_raw0 = widen(0)
+        xt_a0 = turn(a_raw0[:])
+        turn_over(1)
+        group_b(0)
+        group_b(1)
+        quantize_b(0)
+        mixed0 = group_a(0, xt_a0)
+        repeat_b(0, 0, QUAD)
+        grouped0 = scale_a(0, mixed0)
+        repeat_b(0, QUAD, R)
+        codes0, scales0 = quantize_a(0, grouped0)
+        quantize_b(1)
+        b_layer(0, 0, True)
+        b_layer(0, 1, True)
+        a_layer(0, codes0, scales0)
+        b_layer(0, 2, True)
+        b_layer(0, 3, True)
+
+        quads = [(n, s, h) for n in range(NB) for s in range(W) for h in range(2)]
+        last = len(quads)
+        live = {}
+        groups = {}
+
+        def one_read(q):
+            return 1 if q >= last - LATE else 2
+
+        def sums(q, b):
+            n, s, half = quads[q]
+            single = one_read(q)
+            if b == 0:
+                live[q] = {
+                    "pair": work.tile([P, QUAD - single, P, 4], BF16, name="pair", tag="pair"),
+                    "small": work.tile([P, QUAD - single, P, 4], BF16, name="small", tag="small"),
+                    "hidden": work.tile([P, QUAD, P, 4], BF16, name="hidden", tag="hidden", align_bytes=64),
+                }
+            picks = shifts[:].rearrange("q w z -> q (w z)")[:, s * Z : s * Z + P]
+            r = half * QUAD + b
+            x = xps.tile([P, 4, P], F32, name="x", tag="x")
+            for t in range(4):
+                nc.tensor.matmul(
+                    x[:, t, :], lhsT=a_part[:, n, t, :], rhs=ident[:], is_transpose=True, start=True, stop=False
+                )
+                nc.tensor.matmul(
+                    x[:, t, :], lhsT=b_part[:, n, r, t, :], rhs=picks, is_transpose=True, start=False, stop=True
+                )
+            view = x[:].rearrange("m t c -> m c t")
+            if b < single:
+                first = work.tile([P, P, 4], BF16, name="first", tag="first", bufs=8)
+                nc.scalar.copy(out=first[:], in_=view)
+                live[q][b] = (view, first)
+            else:
+                nc.scalar.copy(out=live[q]["pair"][:, b - single], in_=view)
+                nc.scalar.activation(out=live[q]["small"][:, b - single], in_=view, func=COPY, scale=SLOPE)
+
+        def leaky(q, b):
+            view, first = live[q][b]
+            nc.vector.scalar_tensor_tensor(
+                out=live[q]["hidden"][:, b], in0=view, scalar=SLOPE, in1=first[:], op0=ALU.mult, op1=ALU.max
+            )
+
+        def leaky_pair(q):
+            nc.vector.tensor_tensor(
+                out=live[q]["hidden"][:, one_read(q) :], in0=live[q]["pair"][:], in1=live[q]["small"][:], op=ALU.max
+            )
+
+        def quantize(q):
+            hidden = live[q]["hidden"]
+            codes = work.tile([P, QUAD * P], U32, name="codes", tag="codes", align_bytes=64)
+            scales = work.tile([P, QUAD * P], U8, name="scales", tag="scales", align_bytes=64)
+            nc.vector.quantize_mx(
+                out=codes[:].bitcast(FP8X4), scales=scales[:], in_=hidden[:].rearrange("m b c t -> m (b c t)")
+            )
+            live[q] = (codes, scales)
+
+        def second_layer(q):
+            codes, scales = live[q]
+            y = yps.tile([P, QUAD, K1], F32, name="y", tag="y")
+            for b in range(QUAD):
+                cols = slice(b * P, (b + 1) * P)
+                nc.tensor.matmul_mx(
+                    out=y[:, b, :],
+                    lhsT=codes[:, cols].bitcast(FP8X4),
+                    lhsT_scale=scales[:, cols],
+                    rhs=w2[:].bitcast(FP4X4),
+                    rhs_scale=w2_sc[:],
+                    start=True,
+                    stop=True,
+                )
+            live[q] = y
+
+        def add_bias(q):
+            y = live.pop(q)
+            if q % 2 == 0:
+                groups[q // 2] = (
+                    work.tile([P, R, K1], F32, name="z", tag="z", bufs=3),
+                    work.tile([P, R, K1], F32, name="o", tag="o", bufs=16),
+                )
+            z = groups[q // 2][0]
+            half = slice((q % 2) * QUAD, (q % 2 + 1) * QUAD)
+            nc.vector.tensor_tensor(
+                out=z[:, half, :], in0=y[:], in1=b2_all[:].unsqueeze(1).to_broadcast([P, QUAD, K1]), op=ALU.add
+            )
+
+        def finish(g, r0, r1):
+            n, s = divmod(g, W)
+            z, o = groups[g]
+            nc.vector.scalar_tensor_tensor(
+                out=o[:, r0:r1, :], in0=z[:, r0:r1, :], scalar=SLOPE, in1=z[:, r0:r1, :], op0=ALU.mult, op1=ALU.max
+            )
+            for w in range(W):
+                j0 = R * ((w + s) % W)
+                rows = slice(Z * w, Z * (w + 1))
+                nc.sync.dma_start(out=out[n, rows, j0 + r0 : j0 + r1, :], in_=o[rows, r0:r1, :])
+
+        state = {}
+        for q in range(last + 4):
+            if q == 0:
+                sums(0, 0)
+                sums(0, 1)
+                b_layer(0, 4, False)
+                b_layer(0, 5, False)
+                leaky(0, 0)
+                sums(0, 2)
+                b_layer(0, 6, False)
+                leaky(0, 1)
+                sums(0, 3)
+                b_layer(0, 7, False)
+                leaky_pair(0)
+                continue
+            if q < last:
+                for b in range(QUAD):
+                    sums(q, b)
+            if 2 <= q < last + 2:
+                second_layer(q - 2)
+            if q < last:
+                leaky(q, 0)
+            if 1 <= q <= last:
+                quantize(q - 1)
+            if q < last and one_read(q) == 2:
+                leaky(q, 1)
+            if q >= 5 and q % 2 == 1 and q - 4 < last - 2:
+                finish((q - 4) // 2, 0, R)
+            if q == last + 2:
+                finish(last // 2 - 1, 0, QUAD)
+            if 3 <= q < last + 3:
+                add_bias(q - 3)
+            if q == last + 3:
+                finish(last // 2 - 1, QUAD, R)
+            if q < last:
+                leaky_pair(q)
+            if q == 2:
+                park_b()
+            if q == 3:
+                state["raw"] = widen(1)
+            if q == 4:
+                state["mixed"] = group_a(1, turn(state["raw"][:]))
+            if q == 5:
+                state["grouped"] = scale_a(1, state["mixed"])
+            if q == 6:
+                state["codes"] = quantize_a(1, state["grouped"])
+            if q == 7:
+                a_layer(1, state["codes"][0], state["codes"][1])

@@ -18,11 +18,22 @@ P = 128
 NB, NI, NJ, D, K0, K1 = 2, 128, 64, 512, 512, 128
 FLOPS = 2 * (NB * (NI + NJ) * D * K0 + NB * NI * NJ * K0 * K1)
 SLOPE = 0.01
-R = 8
-W = 8
-Z = 16
-QUAD = 4
-LATE = 2
+R = 4
+W = NJ // R
+Z = P // (NB * W)
+M = NB * Z
+H = NB * NI // P
+
+
+def pieces(lo, hi, most):
+    found = []
+    while lo < hi:
+        size = most
+        while size > hi - lo:
+            size = size // 2
+        found.append((lo, size))
+        lo = lo + size
+    return found
 
 
 def tile_matchmatrix_pa_t_w4_kernel(
@@ -37,50 +48,46 @@ def tile_matchmatrix_pa_t_w4_kernel(
         ctx.enter_context(tc.manual_schedule())
 
         b_raw = keep.tile([P, D], BF16, align_bytes=64)
-        nc.sync.dma_start(out=b_raw[:], in_=sent_b.rearrange("n j k -> (n j) k"))
+        a_bytes = keep.tile([P, H * D], U8, align_bytes=64)
         a_scale = keep.tile([P, 4], F32)
-        nc.scalar.dma_start(out=a_scale[:], in_=sent_a_scale.rearrange("x y (p t) -> p (x y t)", t=4))
-        a_bytes = keep.tile([P, NB, D], U8, align_bytes=64)
-        nc.sync.dma_start(out=a_bytes[:], in_=sent_a_bytes.rearrange("n i k -> i n k"))
         b1_all = keep.tile([P, K0], BF16)
-        nc.scalar.dma_start(out=b1_all[:], in_=b1.partition_broadcast(P))
+        b2_all = keep.tile([P, K1], BF16)
         w1 = keep.tile([P, 2, 2 * K0], U8, align_bytes=64)
         w1_sc = keep.tile([P, 2, K0], U8, align_bytes=64)
         w2 = keep.tile([P, 2 * K1], U8, align_bytes=64)
         w2_sc = keep.tile([P, K1], U8, align_bytes=64)
         b_scales = keep.tile([P, P], U8, align_bytes=64)
-        probe = keep.tile([P, 1], F32)
-        idle = keep.tile([P, 4 * P], BF16)
-        nc.vector.memset(idle[:], 0.0)
         nc.vector.memset(w1_sc[:].rearrange("p g n -> p (g n)").bitcast(I32), 0)
-        nc.vector.memset(probe[:], 0.0)
         nc.vector.memset(b_scales[:].bitcast(I32), 0)
         nc.vector.memset(w2_sc[:].bitcast(I32), 0)
-        for g in (1, 0):
-            nc.sync.dma_start(out=w1[:, g, :].bitcast(I32), in_=w1_words[g].bitcast(I32))
+        nc.sync.dma_start(out=b_raw[:], in_=sent_b.rearrange("n j k -> (n j) k"))
+        nc.sync.dma_start(out=a_bytes[:], in_=sent_a_bytes.rearrange("n (x h) k -> (n x) (h k)", h=H))
+        nc.scalar.dma_start(out=a_scale[:], in_=sent_a_scale.rearrange("x y (p t) -> p (x y t)", t=4))
+        nc.sync.dma_start(out=w1[:].bitcast(I32), in_=w1_words.rearrange("g p n -> p g n").bitcast(I32))
         for q in range(4):
             nc.sync.dma_start(
                 out=w1_sc[32 * q : 32 * q + 4, :, :].bitcast(I32),
                 in_=w1_scales[:, 4 * q : 4 * q + 4, :].rearrange("g q n -> q g n").bitcast(I32),
             )
-        warm = keep.tile([P, 1], F32)
-        nc.scalar.activation(out=warm[:], in_=probe[:], func=COPY, scale=SLOPE)
-        b2_all = keep.tile([P, K1], BF16)
-        nc.sync.dma_start(out=b2_all[:], in_=b2.partition_broadcast(P))
+        nc.sync.dma_start(out=b1_all[:], in_=b1.partition_broadcast(P))
         nc.sync.dma_start(out=w2[:].bitcast(I32), in_=w2_words[0].bitcast(I32))
         for q in range(4):
             nc.sync.dma_start(
                 out=w2_sc[32 * q : 32 * q + 4, :].bitcast(I32),
                 in_=w2_scales[0, 4 * q : 4 * q + 4, :].bitcast(I32),
             )
+        nc.sync.dma_start(out=b2_all[:], in_=b2.partition_broadcast(P))
 
         ident = keep.tile([P, P], F32)
         make_identity(nc, ident[:])
-        shifts = keep.tile([P, 2 * W, Z], F32)
+        shifts = keep.tile([P, 2 * W, M], F32)
         for half in range(2):
             nc.vector.tensor_copy(
-                out=shifts[:, half * W : (half + 1) * W, :], in_=ident[:].rearrange("q (z w) -> q w z", w=W)
+                out=shifts[:, half * W : (half + 1) * W, :], in_=ident[:].rearrange("q (m w) -> q w m", w=W)
             )
+
+        def picks(s):
+            return shifts[:].rearrange("q w m -> q (w m)")[:, s * M : s * M + P]
 
         def turn(raw):
             words = raw.bitcast(F32)
@@ -89,60 +96,34 @@ def tile_matchmatrix_pa_t_w4_kernel(
                 nc.tensor.transpose(xt[:, u, :], words[:, u : 2 * P : 2], ident[:])
             return xt
 
-        def widen(n):
-            a_raw = keep.tile([P, D], BF16, align_bytes=64, name=f"a_raw{n}")
-            nc.scalar.copy(out=a_raw[:], in_=a_bytes[:, n, :].bitcast(FP8))
-            return a_raw
-
-        b_grouped = keep.tile([P, P, 4], BF16, align_bytes=64)
+        a_raw = keep.tile([P, H * D], BF16, align_bytes=64)
+        b_grouped = keep.tile([P, P * 4], BF16, align_bytes=64)
         b_codes = keep.tile([P, P], U32, align_bytes=64)
-        rep_codes = keep.tile([P, NB, R, Z, W], U32, align_bytes=64)
-        rep_scales = keep.tile([P, NB, R, Z, W], U8, align_bytes=64)
+        rep_codes = keep.tile([P, R * P], U32, align_bytes=64)
+        rep_scales = keep.tile([P, R * P], U8, align_bytes=64)
+        a_part = [keep.tile([P, 4, P], F32, name=f"a_part{h}") for h in range(H)]
+        b_part = [keep.tile([P, 4, P], F32, name=f"b_part{r}") for r in range(R)]
 
-        def repeat_b(n, r0, r1):
-            cols = slice(n * NJ + r0 * W, n * NJ + r1 * W)
-            nr = r1 - r0
-            nc.vector.tensor_copy(
-                out=rep_codes[:, n, r0:r1].rearrange("p r z w -> p (r z w)").bitcast(I32).rearrange("p (r z w) -> p r z w", r=nr, z=Z),
-                in_=b_codes[:, cols].bitcast(I32).rearrange("p (r w) -> p r w", r=nr).unsqueeze(2).to_broadcast([P, nr, Z, W]),
-            )
-            nc.vector.tensor_copy(
-                out=rep_scales[:, n, r0:r1].rearrange("p r z w -> p (r z w)").bitcast(I32).rearrange("p (r z w) -> p r z w", r=nr, z=Z),
-                in_=b_scales[:, cols]
-                .bitcast(I32)
-                .rearrange("p (r w) -> p r w", r=nr)
-                .unsqueeze(2)
-                .to_broadcast([P, nr, Z, W // 4]),
-            )
-
-        def group_a(n, xt):
-            a_mixed = keep.tile([P, P, 4], BF16, align_bytes=64, name=f"a_mixed{n}")
-            nc.scalar.copy(
-                out=a_mixed[:].rearrange("p c t -> p (c t)").bitcast(F32).rearrange("p (c u) -> p c u", u=2),
-                in_=xt[:].rearrange("p u c -> p c u"),
-            )
-            return a_mixed
-
-        def scale_a(n, a_mixed):
-            a_grouped = keep.tile([P, P, 4], BF16, align_bytes=64, name=f"a_grouped{n}")
+        def scale_a(h, xt):
+            a_grouped = keep.tile([P, P, 2, 2], BF16, align_bytes=64, name=f"a_grouped{h}")
             nc.vector.tensor_tensor(
-                out=a_grouped[:], in0=a_mixed[:], in1=a_scale[:].unsqueeze(1).to_broadcast([P, P, 4]), op=ALU.mult
+                out=a_grouped[:],
+                in0=xt[:].rearrange("p u c -> p (u c)").bitcast(BF16).rearrange("p (u c e) -> p c u e", u=2, e=2),
+                in1=a_scale[:].rearrange("p (u e) -> p u e", u=2).unsqueeze(1).to_broadcast([P, P, 2, 2]),
+                op=ALU.mult,
             )
             return a_grouped
 
-        def quantize_a(n, a_grouped):
-            a_codes = keep.tile([P, P], U32, align_bytes=64, name=f"a_codes{n}")
-            a_scales = keep.tile([P, P], U8, align_bytes=64, name=f"a_scales{n}")
+        def quantize_a(h, a_grouped):
+            a_codes = keep.tile([P, P], U32, align_bytes=64, name=f"a_codes{h}")
+            a_scales = keep.tile([P, P], U8, align_bytes=64, name=f"a_scales{h}")
             nc.vector.quantize_mx(
-                out=a_codes[:].bitcast(FP8X4), scales=a_scales[:], in_=a_grouped[:].rearrange("p c t -> p (c t)")
+                out=a_codes[:].bitcast(FP8X4), scales=a_scales[:], in_=a_grouped[:].rearrange("p c u e -> p (c u e)")
             )
             return a_codes, a_scales
 
-        a_part = keep.tile([P, NB, 4, P], F32)
-        b_part = keep.tile([P, NB, R, 4, P], F32)
-
-        def a_layer(n, a_codes, a_scales):
-            pa = xps.tile([P, K0], F32, name="pa", tag="x")
+        def a_product(a_codes, a_scales):
+            pa = yps.tile([P, K0], F32, name="pa", tag="y")
             nc.tensor.matmul_mx(
                 out=pa[:],
                 lhsT=a_codes[:].bitcast(FP8X4),
@@ -152,240 +133,204 @@ def tile_matchmatrix_pa_t_w4_kernel(
                 start=True,
                 stop=True,
             )
+            return pa
+
+        def a_rows(h, pa):
             nc.vector.tensor_tensor(
-                out=a_part[:, n],
+                out=a_part[h][:],
                 in0=pa[:].rearrange("i (m t) -> i t m", t=4),
                 in1=b1_all[:].rearrange("i (m t) -> i t m", t=4),
                 op=ALU.add,
             )
 
-        def b_layer(n, r, scalar):
+        def b_layer(r):
             pb = xps.tile([P, K0], F32, name="pb", tag="x")
+            cols = slice(r * P, (r + 1) * P)
             nc.tensor.matmul_mx(
                 out=pb[:],
-                lhsT=rep_codes[:, n, r].rearrange("p z w -> p (z w)").bitcast(FP8X4),
-                lhsT_scale=rep_scales[:, n, r].rearrange("p z w -> p (z w)"),
+                lhsT=rep_codes[:, cols].bitcast(FP8X4),
+                lhsT_scale=rep_scales[:, cols],
                 rhs=w1[:, 1, :].bitcast(FP4X4),
                 rhs_scale=w1_sc[:, 1, :],
                 start=True,
                 stop=True,
             )
-            dst = b_part[:, n, r]
-            view = pb[:].rearrange("q (m t) -> q t m", t=4)
-            if scalar:
-                nc.scalar.copy(out=dst, in_=view)
-            else:
-                nc.vector.tensor_copy(out=dst, in_=view)
+            nc.scalar.copy(out=b_part[r][:], in_=pb[:].rearrange("q (m t) -> q t m", t=4))
 
-        def park_b():
-            pb = xps.tile([P, K0], F32, name="pb", tag="x")
-            nc.tensor.matmul_mx(
-                out=pb[:],
-                lhsT=b_codes[:].bitcast(FP8X4),
-                lhsT_scale=b_scales[:],
-                rhs=w1[:, 1, :].bitcast(FP4X4),
-                rhs_scale=w1_sc[:, 1, :],
-                start=True,
-                stop=True,
-            )
-            b_rows = keep.tile([P, 4, P], F32)
-            nc.scalar.copy(out=b_rows[:], in_=pb[:].rearrange("q (m t) -> q t m", t=4))
-            park = out[1, 120:124].rearrange("i j k -> (i j k)")
-            nc.sync.dma_start(
-                out=park.rearrange("(j c) -> j c", c=K0), in_=b_rows[NJ:, :, :].rearrange("j t m -> j (t m)")
-            )
-            rows = park.rearrange("(r w c) -> w r c", r=R, w=W)
-            for w in range(W):
-                nc.sync.dma_start(
-                    out=b_part[w::W, 1].rearrange("q r t m -> q r (t m)"), in_=rows[w].partition_broadcast(Z)
-                )
-
-        spin = yps.tile([P, 4 * P], F32, name="spin", tag="y")
-
-        def turn_over(times):
-            for i in range(times):
-                nc.tensor.matmul(spin[:], lhsT=idle[:, :P], rhs=idle[:], start=True, stop=True)
-
-        def group_b(n):
-            half = slice(n * NJ, (n + 1) * NJ)
-            nc.vector.tensor_copy(
-                out=b_grouped[:, half, :]
-                .rearrange("p c t -> p (c t)")
-                .bitcast(F32)
-                .rearrange("p (r w u) -> p r w u", r=R, w=W),
-                in_=xt_b[:, :, half].rearrange("p u (w r) -> p r w u", r=R),
-            )
-
-        def quantize_b(n):
-            half = slice(n * NJ, (n + 1) * NJ)
-            nc.vector.quantize_mx(
-                out=b_codes[:, half].bitcast(FP8X4),
-                scales=b_scales[:, half],
-                in_=b_grouped[:, half, :].rearrange("p c t -> p (c t)"),
-            )
-
-        turn_over(3)
-        xt_b = turn(b_raw[:])
-        turn_over(2)
-        a_raw0 = widen(0)
-        xt_a0 = turn(a_raw0[:])
-        turn_over(1)
-        group_b(0)
-        group_b(1)
-        quantize_b(0)
-        mixed0 = group_a(0, xt_a0)
-        repeat_b(0, 0, QUAD)
-        grouped0 = scale_a(0, mixed0)
-        repeat_b(0, QUAD, R)
-        codes0, scales0 = quantize_a(0, grouped0)
-        quantize_b(1)
-        b_layer(0, 0, True)
-        b_layer(0, 1, True)
-        a_layer(0, codes0, scales0)
-        b_layer(0, 2, True)
-        b_layer(0, 3, True)
-
-        quads = [(n, s, h) for n in range(NB) for s in range(W) for h in range(2)]
+        quads = [(h, W - 1 - s) for h in range(H) for s in range(W)]
         last = len(quads)
         live = {}
         groups = {}
 
         def one_read(q):
-            return 1 if q >= last - LATE else 2
+            if q < 2:
+                return 4
+            if q == 2:
+                return 3
+            if q == last - 3:
+                return 1
+            if q > last - 3:
+                return 0
+            return 2
 
-        def sums(q, b):
-            n, s, half = quads[q]
+        def sums(q, r):
+            h, s = quads[q]
             single = one_read(q)
-            if b == 0:
-                live[q] = {
-                    "pair": work.tile([P, QUAD - single, P, 4], BF16, name="pair", tag="pair"),
-                    "small": work.tile([P, QUAD - single, P, 4], BF16, name="small", tag="small"),
-                    "hidden": work.tile([P, QUAD, P, 4], BF16, name="hidden", tag="hidden", align_bytes=64),
-                }
-            picks = shifts[:].rearrange("q w z -> q (w z)")[:, s * Z : s * Z + P]
-            r = half * QUAD + b
+            if r == 0:
+                live[q] = {"hidden": work.tile([P, R, P, 4], BF16, name="hidden", tag="hidden", align_bytes=64)}
+                if single < R:
+                    live[q]["pair"] = work.tile([P, R - single, P, 4], BF16, name="pair", tag="pair")
+                    live[q]["small"] = work.tile([P, R - single, P, 4], BF16, name="small", tag="small")
             x = xps.tile([P, 4, P], F32, name="x", tag="x")
             for t in range(4):
                 nc.tensor.matmul(
-                    x[:, t, :], lhsT=a_part[:, n, t, :], rhs=ident[:], is_transpose=True, start=True, stop=False
+                    x[:, t, :], lhsT=a_part[h][:, t, :], rhs=picks(0), is_transpose=True, start=True, stop=False
                 )
                 nc.tensor.matmul(
-                    x[:, t, :], lhsT=b_part[:, n, r, t, :], rhs=picks, is_transpose=True, start=False, stop=True
+                    x[:, t, :], lhsT=b_part[r][:, t, :], rhs=picks(s), is_transpose=True, start=False, stop=True
                 )
             view = x[:].rearrange("m t c -> m c t")
-            if b < single:
+            if r < single:
                 first = work.tile([P, P, 4], BF16, name="first", tag="first", bufs=8)
                 nc.scalar.copy(out=first[:], in_=view)
-                live[q][b] = (view, first)
+                live[q][r] = (view, first)
             else:
-                nc.scalar.copy(out=live[q]["pair"][:, b - single], in_=view)
-                nc.scalar.activation(out=live[q]["small"][:, b - single], in_=view, func=COPY, scale=SLOPE)
+                nc.scalar.copy(out=live[q]["pair"][:, r - single], in_=view)
+                nc.scalar.activation(out=live[q]["small"][:, r - single], in_=view, func=COPY, scale=SLOPE)
 
-        def leaky(q, b):
-            view, first = live[q][b]
+        def leaky(q, r):
+            view, first = live[q][r]
             nc.vector.scalar_tensor_tensor(
-                out=live[q]["hidden"][:, b], in0=view, scalar=SLOPE, in1=first[:], op0=ALU.mult, op1=ALU.max
+                out=live[q]["hidden"][:, r], in0=view, scalar=SLOPE, in1=first[:], op0=ALU.mult, op1=ALU.max
             )
 
-        def leaky_pair(q):
+        def leaky_pair(q, r0, r1):
+            single = one_read(q)
+            part = slice(r0 - single, r1 - single)
             nc.vector.tensor_tensor(
-                out=live[q]["hidden"][:, one_read(q) :], in0=live[q]["pair"][:], in1=live[q]["small"][:], op=ALU.max
+                out=live[q]["hidden"][:, r0:r1], in0=live[q]["pair"][:, part], in1=live[q]["small"][:, part], op=ALU.max
             )
 
-        def quantize(q):
-            hidden = live[q]["hidden"]
-            codes = work.tile([P, QUAD * P], U32, name="codes", tag="codes", align_bytes=64)
-            scales = work.tile([P, QUAD * P], U8, name="scales", tag="scales", align_bytes=64)
+        def quantize(q, r0, r1):
+            if r0 == 0:
+                live[q]["codes"] = work.tile([P, R * P], U32, name="codes", tag="codes", align_bytes=64)
+                live[q]["scales"] = work.tile([P, R * P], U8, name="scales", tag="scales", align_bytes=64)
+            cols = slice(r0 * P, r1 * P)
             nc.vector.quantize_mx(
-                out=codes[:].bitcast(FP8X4), scales=scales[:], in_=hidden[:].rearrange("m b c t -> m (b c t)")
+                out=live[q]["codes"][:, cols].bitcast(FP8X4),
+                scales=live[q]["scales"][:, cols],
+                in_=live[q]["hidden"][:, r0:r1].rearrange("m b c t -> m (b c t)"),
             )
-            live[q] = (codes, scales)
 
         def second_layer(q):
-            codes, scales = live[q]
-            y = yps.tile([P, QUAD, K1], F32, name="y", tag="y")
-            for b in range(QUAD):
-                cols = slice(b * P, (b + 1) * P)
+            y = yps.tile([P, R, K1], F32, name="y", tag="y")
+            for r in range(R):
+                cols = slice(r * P, (r + 1) * P)
                 nc.tensor.matmul_mx(
-                    out=y[:, b, :],
-                    lhsT=codes[:, cols].bitcast(FP8X4),
-                    lhsT_scale=scales[:, cols],
+                    out=y[:, r, :],
+                    lhsT=live[q]["codes"][:, cols].bitcast(FP8X4),
+                    lhsT_scale=live[q]["scales"][:, cols],
                     rhs=w2[:].bitcast(FP4X4),
                     rhs_scale=w2_sc[:],
                     start=True,
                     stop=True,
                 )
-            live[q] = y
+            live[q]["y"] = y
 
         def add_bias(q):
-            y = live.pop(q)
             if q % 2 == 0:
                 groups[q // 2] = (
-                    work.tile([P, R, K1], F32, name="z", tag="z", bufs=3),
-                    work.tile([P, R, K1], F32, name="o", tag="o", bufs=16),
+                    work.tile([P, 2, R, K1], F32, name="z", tag="z", bufs=3),
+                    work.tile([P, 2, R, K1], F32, name="o", tag="o", bufs=4),
                 )
-            z = groups[q // 2][0]
-            half = slice((q % 2) * QUAD, (q % 2 + 1) * QUAD)
             nc.vector.tensor_tensor(
-                out=z[:, half, :], in0=y[:], in1=b2_all[:].unsqueeze(1).to_broadcast([P, QUAD, K1]), op=ALU.add
+                out=groups[q // 2][0][:, q % 2],
+                in0=live.pop(q)["y"][:],
+                in1=b2_all[:].unsqueeze(1).to_broadcast([P, R, K1]),
+                op=ALU.add,
             )
 
-        def finish(g, r0, r1):
-            n, s = divmod(g, W)
-            z, o = groups[g]
+        rows = out.rearrange("n (z x) j k -> (n z) (x j k)", z=Z)
+        span = rows.shape[1]
+        step = H * NJ * K1 + R * K1
+
+        def store(q, o):
+            h, s = quads[q]
+            for lo, hi, back in ((0, W - s, 0), (W - s, W, NJ * K1)):
+                for w0, nw in pieces(lo, hi, W // 2):
+                    base = w0 * step + h * NJ * K1 + s * R * K1 - back
+                    early = max(0, base + nw * step - span)
+                    window = rows[:, base - early : base - early + nw * step].rearrange("m (w x) -> w m x", x=step)
+                    nc.sync.dma_start(
+                        out=window[:, :, early : early + R * K1],
+                        in_=o[w0 * M : (w0 + nw) * M].rearrange("c r k -> c (r k)"),
+                    )
+
+        def finish(q0, q1):
+            z, o = groups[q0 // 2]
+            part = slice(q0 % 2, q0 % 2 + q1 - q0)
             nc.vector.scalar_tensor_tensor(
-                out=o[:, r0:r1, :], in0=z[:, r0:r1, :], scalar=SLOPE, in1=z[:, r0:r1, :], op0=ALU.mult, op1=ALU.max
+                out=o[:, part], in0=z[:, part], scalar=SLOPE, in1=z[:, part], op0=ALU.mult, op1=ALU.max
             )
-            for w in range(W):
-                j0 = R * ((w + s) % W)
-                rows = slice(Z * w, Z * (w + 1))
-                nc.sync.dma_start(out=out[n, rows, j0 + r0 : j0 + r1, :], in_=o[rows, r0:r1, :])
+            for q in range(q0, q1):
+                store(q, o[:, q % 2])
 
-        state = {}
-        for q in range(last + 4):
-            if q == 0:
-                sums(0, 0)
-                sums(0, 1)
-                b_layer(0, 4, False)
-                b_layer(0, 5, False)
-                leaky(0, 0)
-                sums(0, 2)
-                b_layer(0, 6, False)
-                leaky(0, 1)
-                sums(0, 3)
-                b_layer(0, 7, False)
-                leaky_pair(0)
-                continue
+        xt_b = turn(b_raw[:])
+        nc.vector.tensor_copy(out=a_raw[:], in_=a_bytes[:].bitcast(FP8))
+        xt_a = [turn(a_raw[:, h * D : (h + 1) * D]) for h in range(H)]
+        nc.scalar.copy(
+            out=b_grouped[:].bitcast(F32).rearrange("p (r c u) -> p r c u", r=R, u=2),
+            in_=xt_b[:].rearrange("p u (c r) -> p r c u", r=R),
+        )
+        nc.vector.quantize_mx(out=b_codes[:].bitcast(FP8X4), scales=b_scales[:], in_=b_grouped[:])
+        grouped0 = scale_a(0, xt_a[0])
+        nc.vector.tensor_copy(
+            out=rep_codes[:].bitcast(I32).rearrange("p (g z w) -> p g z w", z=Z, w=W),
+            in_=b_codes[:].bitcast(I32).rearrange("p (g w) -> p g w", w=W).unsqueeze(2).to_broadcast([P, R * NB, Z, W]),
+        )
+        nc.vector.tensor_copy(
+            out=rep_scales[:].bitcast(I32).rearrange("p (g z w) -> p g z w", z=Z, w=W // 4),
+            in_=b_scales[:]
+            .bitcast(I32)
+            .rearrange("p (g w) -> p g w", w=W // 4)
+            .unsqueeze(2)
+            .to_broadcast([P, R * NB, Z, W // 4]),
+        )
+        quantized0 = quantize_a(0, grouped0)
+        grouped1 = scale_a(1, xt_a[1])
+        b_layer(0)
+        pa0 = a_product(*quantized0)
+        b_layer(1)
+        b_layer(2)
+        a_rows(0, pa0)
+        quantized1 = quantize_a(1, grouped1)
+        b_layer(3)
+        sums(0, 0)
+        a_rows(1, a_product(*quantized1))
+
+        for q in range(last + 3):
+            single = one_read(q) if q < last else 0
             if q < last:
-                for b in range(QUAD):
-                    sums(q, b)
+                for r in range(1 if q == 0 else 0, R):
+                    sums(q, r)
             if 2 <= q < last + 2:
                 second_layer(q - 2)
-            if q < last:
+            if single > 0:
                 leaky(q, 0)
             if 1 <= q <= last:
-                quantize(q - 1)
-            if q < last and one_read(q) == 2:
-                leaky(q, 1)
+                quantize(q - 1, 0, R)
+            for r in range(1, single):
+                leaky(q, r)
             if q >= 5 and q % 2 == 1 and q - 4 < last - 2:
-                finish((q - 4) // 2, 0, R)
+                finish(q - 5, q - 3)
+            if q < last and single == 0:
+                leaky_pair(q, 0, R // 2)
             if q == last + 2:
-                finish(last // 2 - 1, 0, QUAD)
-            if 3 <= q < last + 3:
+                finish(last - 2, last - 1)
+            if 3 <= q:
                 add_bias(q - 3)
-            if q == last + 3:
-                finish(last // 2 - 1, QUAD, R)
-            if q < last:
-                leaky_pair(q)
-            if q == 2:
-                park_b()
-            if q == 3:
-                state["raw"] = widen(1)
-            if q == 4:
-                state["mixed"] = group_a(1, turn(state["raw"][:]))
-            if q == 5:
-                state["grouped"] = scale_a(1, state["mixed"])
-            if q == 6:
-                state["codes"] = quantize_a(1, state["grouped"])
-            if q == 7:
-                a_layer(1, state["codes"][0], state["codes"][1])
+            if q < last and single == 0:
+                leaky_pair(q, R // 2, R)
+            elif q < last and single < R:
+                leaky_pair(q, single, R)
+        finish(last - 1, last)

@@ -159,28 +159,18 @@ def tile_matchmatrix_pa_t_w4_kernel(
 
         quads = [(h, W - 1 - s) for h in range(H) for s in range(W)]
         last = len(quads)
+        units = [[0]] + [[q, q + 1] for q in range(1, last - 3, 2)] + [[q] for q in range(last - 3, last)]
+        twice = [0, 2, 3] + [R] * (len(units) - 3)
         live = {}
-        groups = {}
 
-        def one_read(q):
-            if q < 2:
-                return 4
-            if q == 2:
-                return 3
-            if q == last - 3:
-                return 1
-            if q > last - 3:
-                return 0
-            return 2
-
-        def sums(q, r):
-            h, s = quads[q]
-            single = one_read(q)
-            if r == 0:
-                live[q] = {"hidden": work.tile([P, R, P, 4], BF16, name="hidden", tag="hidden", align_bytes=64)}
-                if single < R:
-                    live[q]["pair"] = work.tile([P, R - single, P, 4], BF16, name="pair", tag="pair")
-                    live[q]["small"] = work.tile([P, R - single, P, 4], BF16, name="small", tag="small")
+        def sums(k, b):
+            h, s = quads[units[k][b // R]]
+            r = b % R
+            if b == 0:
+                live[k] = {"hidden": work.tile([P, 2 * R, P, 4], BF16, name="hidden", tag="hidden", align_bytes=64, bufs=3)}
+                if twice[k] > 0:
+                    live[k]["pair"] = work.tile([P, R, P, 4], BF16, name="pair", tag="pair", bufs=2)
+                    live[k]["small"] = work.tile([P, R, P, 4], BF16, name="small", tag="small", bufs=2)
             x = xps.tile([P, 4, P], F32, name="x", tag="x")
             for t in range(4):
                 nc.tensor.matmul(
@@ -190,63 +180,59 @@ def tile_matchmatrix_pa_t_w4_kernel(
                     x[:, t, :], lhsT=b_part[r][:, t, :], rhs=picks(s), is_transpose=True, start=False, stop=True
                 )
             view = x[:].rearrange("m t c -> m c t")
-            if r < single:
+            if b >= twice[k]:
                 first = work.tile([P, P, 4], BF16, name="first", tag="first", bufs=8)
                 nc.scalar.copy(out=first[:], in_=view)
-                live[q][r] = (view, first)
+                live[k][b] = (view, first)
             else:
-                nc.scalar.copy(out=live[q]["pair"][:, r - single], in_=view)
-                nc.scalar.activation(out=live[q]["small"][:, r - single], in_=view, func=COPY, scale=SLOPE)
+                nc.scalar.copy(out=live[k]["pair"][:, b], in_=view)
+                nc.scalar.activation(out=live[k]["small"][:, b], in_=view, func=COPY, scale=SLOPE)
 
-        def leaky(q, r):
-            view, first = live[q][r]
+        def leaky(k, b):
+            view, first = live[k][b]
             nc.vector.scalar_tensor_tensor(
-                out=live[q]["hidden"][:, r], in0=view, scalar=SLOPE, in1=first[:], op0=ALU.mult, op1=ALU.max
+                out=live[k]["hidden"][:, b], in0=view, scalar=SLOPE, in1=first[:], op0=ALU.mult, op1=ALU.max
             )
 
-        def leaky_pair(q, r0, r1):
-            single = one_read(q)
-            part = slice(r0 - single, r1 - single)
+        def leaky_pair(k, b0, b1):
             nc.vector.tensor_tensor(
-                out=live[q]["hidden"][:, r0:r1], in0=live[q]["pair"][:, part], in1=live[q]["small"][:, part], op=ALU.max
+                out=live[k]["hidden"][:, b0:b1], in0=live[k]["pair"][:, b0:b1], in1=live[k]["small"][:, b0:b1], op=ALU.max
             )
 
-        def quantize(q, r0, r1):
-            if r0 == 0:
-                live[q]["codes"] = work.tile([P, R * P], U32, name="codes", tag="codes", align_bytes=64)
-                live[q]["scales"] = work.tile([P, R * P], U8, name="scales", tag="scales", align_bytes=64)
-            cols = slice(r0 * P, r1 * P)
+        def quantize(k, b0, b1):
+            if b0 == 0:
+                live[k]["codes"] = work.tile([P, 2 * R * P], U32, name="codes", tag="codes", align_bytes=64, bufs=3)
+                live[k]["scales"] = work.tile([P, 2 * R * P], U8, name="scales", tag="scales", align_bytes=64, bufs=3)
+            cols = slice(b0 * P, b1 * P)
             nc.vector.quantize_mx(
-                out=live[q]["codes"][:, cols].bitcast(FP8X4),
-                scales=live[q]["scales"][:, cols],
-                in_=live[q]["hidden"][:, r0:r1].rearrange("m b c t -> m (b c t)"),
+                out=live[k]["codes"][:, cols].bitcast(FP8X4),
+                scales=live[k]["scales"][:, cols],
+                in_=live[k]["hidden"][:, b0:b1].rearrange("m b c t -> m (b c t)"),
             )
 
-        def second_layer(q):
+        def second_layer(k, b0, b1):
             y = yps.tile([P, R, K1], F32, name="y", tag="y")
-            for r in range(R):
-                cols = slice(r * P, (r + 1) * P)
+            for b in range(b0, b1):
+                cols = slice(b * P, (b + 1) * P)
                 nc.tensor.matmul_mx(
-                    out=y[:, r, :],
-                    lhsT=live[q]["codes"][:, cols].bitcast(FP8X4),
-                    lhsT_scale=live[q]["scales"][:, cols],
+                    out=y[:, b - b0, :],
+                    lhsT=live[k]["codes"][:, cols].bitcast(FP8X4),
+                    lhsT_scale=live[k]["scales"][:, cols],
                     rhs=w2[:].bitcast(FP4X4),
                     rhs_scale=w2_sc[:],
                     start=True,
                     stop=True,
                 )
-            live[q]["y"] = y
+            live[k]["y", b0] = y
 
-        def add_bias(q):
-            if q % 2 == 0:
-                groups[q // 2] = (
-                    work.tile([P, 2, R, K1], F32, name="z", tag="z", bufs=3),
-                    work.tile([P, 2, R, K1], F32, name="o", tag="o", bufs=4),
-                )
+        def add_bias(k, b0, b1):
+            if b0 == 0:
+                live[k]["z"] = work.tile([P, 2 * R, K1], F32, name="z", tag="z", bufs=2)
+                live[k]["o"] = work.tile([P, 2 * R, K1], F32, name="o", tag="o", bufs=4)
             nc.vector.tensor_tensor(
-                out=groups[q // 2][0][:, q % 2],
-                in0=live.pop(q)["y"][:],
-                in1=b2_all[:].unsqueeze(1).to_broadcast([P, R, K1]),
+                out=live[k]["z"][:, b0:b1],
+                in0=live[k]["y", b0][:, : b1 - b0],
+                in1=b2_all[:].unsqueeze(1).to_broadcast([P, b1 - b0, K1]),
                 op=ALU.add,
             )
 
@@ -254,7 +240,7 @@ def tile_matchmatrix_pa_t_w4_kernel(
         span = rows.shape[1]
         step = H * NJ * K1 + R * K1
 
-        def store(q, o):
+        def store(q, o, r0, r1):
             h, s = quads[q]
             for lo, hi, back in ((0, W - s, 0), (W - s, W, NJ * K1)):
                 for w0, nw in pieces(lo, hi, W // 2):
@@ -262,18 +248,18 @@ def tile_matchmatrix_pa_t_w4_kernel(
                     early = max(0, base + nw * step - span)
                     window = rows[:, base - early : base - early + nw * step].rearrange("m (w x) -> w m x", x=step)
                     nc.sync.dma_start(
-                        out=window[:, :, early : early + R * K1],
+                        out=window[:, :, early + r0 * K1 : early + r1 * K1],
                         in_=o[w0 * M : (w0 + nw) * M].rearrange("c r k -> c (r k)"),
                     )
 
-        def finish(q0, q1):
-            z, o = groups[q0 // 2]
-            part = slice(q0 % 2, q0 % 2 + q1 - q0)
+        def finish(k, b0, b1):
+            z, o = live[k]["z"], live[k]["o"]
             nc.vector.scalar_tensor_tensor(
-                out=o[:, part], in0=z[:, part], scalar=SLOPE, in1=z[:, part], op0=ALU.mult, op1=ALU.max
+                out=o[:, b0:b1], in0=z[:, b0:b1], scalar=SLOPE, in1=z[:, b0:b1], op0=ALU.mult, op1=ALU.max
             )
-            for q in range(q0, q1):
-                store(q, o[:, q % 2])
+            for b in range(b0, b1, R):
+                end = min(b + R, b1)
+                store(units[k][b // R], o[:, b:end], b % R, b % R + end - b)
 
         xt_b = turn(b_raw[:])
         nc.vector.tensor_copy(out=a_raw[:], in_=a_bytes[:].bitcast(FP8))
@@ -308,29 +294,37 @@ def tile_matchmatrix_pa_t_w4_kernel(
         sums(0, 0)
         a_rows(1, a_product(*quantized1))
 
-        for q in range(last + 3):
-            single = one_read(q) if q < last else 0
-            if q < last:
-                for r in range(1 if q == 0 else 0, R):
-                    sums(q, r)
-            if 2 <= q < last + 2:
-                second_layer(q - 2)
-            if single > 0:
-                leaky(q, 0)
-            if 1 <= q <= last:
-                quantize(q - 1, 0, R)
-            for r in range(1, single):
-                leaky(q, r)
-            if q >= 5 and q % 2 == 1 and q - 4 < last - 2:
-                finish(q - 5, q - 3)
-            if q < last and single == 0:
-                leaky_pair(q, 0, R // 2)
-            if q == last + 2:
-                finish(last - 2, last - 1)
-            if 3 <= q:
-                add_bias(q - 3)
-            if q < last and single == 0:
-                leaky_pair(q, R // 2, R)
-            elif q < last and single < R:
-                leaky_pair(q, single, R)
-        finish(last - 1, last)
+        for k in range(len(units)):
+            blocks = R * len(units[k])
+            old = range(0, R * len(units[k - 2]), R) if k >= 2 else []
+            for b in range(1 if k == 0 else 0, blocks):
+                sums(k, b)
+                if b == 1:
+                    for b0 in old:
+                        second_layer(k - 2, b0, b0 + R)
+            if k >= 2:
+                leaky_pair(k - 1, 0, twice[k - 1])
+            for b0 in old:
+                add_bias(k - 2, b0, b0 + R)
+            if k >= 1:
+                quantize(k - 1, 0, R * len(units[k - 1]))
+            if k >= 2:
+                finish(k - 2, 0, R * len(units[k - 2]))
+            for b in range(twice[k], blocks):
+                leaky(k, b)
+
+        end = len(units) - 1
+        half = R // 2
+        second_layer(end - 1, 0, R)
+        leaky_pair(end, 0, half)
+        add_bias(end - 1, 0, R)
+        quantize(end, 0, half)
+        second_layer(end, 0, half)
+        finish(end - 1, 0, R)
+        leaky_pair(end, half, R)
+        add_bias(end, 0, half)
+        quantize(end, half, R)
+        second_layer(end, half, R)
+        finish(end, 0, half)
+        add_bias(end, half, R)
+        finish(end, half, R)

@@ -25,17 +25,6 @@ M = NB * Z
 H = NB * NI // P
 
 
-def pieces(lo, hi, most):
-    found = []
-    while lo < hi:
-        size = most
-        while size > hi - lo:
-            size = size // 2
-        found.append((lo, size))
-        lo = lo + size
-    return found
-
-
 def tile_matchmatrix_pa_t_w4_kernel(
     tc, sent_a_bytes, sent_a_scale, sent_b, w1_words, w1_scales, b1, w2_words, w2_scales, b2, out
 ):
@@ -157,7 +146,8 @@ def tile_matchmatrix_pa_t_w4_kernel(
             )
             nc.scalar.copy(out=b_part[r][:], in_=pb[:].rearrange("q (m t) -> q t m", t=4))
 
-        quads = [(h, W - 1 - s) for h in range(H) for s in range(W)]
+        shift_order = [s for s in range(W) if s % (W // 2)] + [W // 2, 0]
+        quads = [(h, s) for h in range(H) for s in shift_order]
         last = len(quads)
         units = [[0]] + [[q, q + 1] for q in range(1, last - 3, 2)] + [[q] for q in range(last - 3, last)]
         twice = [0, 2, 3] + [R] * (len(units) - 3)
@@ -242,15 +232,15 @@ def tile_matchmatrix_pa_t_w4_kernel(
 
         def store(q, o, r0, r1):
             h, s = quads[q]
-            for lo, hi, back in ((0, W - s, 0), (W - s, W, NJ * K1)):
-                for w0, nw in pieces(lo, hi, W // 2):
-                    base = w0 * step + h * NJ * K1 + s * R * K1 - back
-                    early = max(0, base + nw * step - span)
-                    window = rows[:, base - early : base - early + nw * step].rearrange("m (w x) -> w m x", x=step)
-                    nc.sync.dma_start(
-                        out=window[:, :, early + r0 * K1 : early + r1 * K1],
-                        in_=o[w0 * M : (w0 + nw) * M].rearrange("c r k -> c (r k)"),
-                    )
+            cut = W - s if s else W // 2
+            for w0, nw in ((0, cut), (cut, W - cut)):
+                base = w0 * step + h * NJ * K1 + s * R * K1 - (NJ * K1 if w0 + s >= W else 0)
+                early = max(0, base + nw * step - span)
+                window = rows[:, base - early : base - early + nw * step].rearrange("m (w x) -> w m x", x=step)
+                nc.sync.dma_start(
+                    out=window[:, :, early + r0 * K1 : early + r1 * K1],
+                    in_=o[w0 * M : (w0 + nw) * M].rearrange("c r k -> c (r k)"),
+                )
 
         def finish(k, b0, b1):
             z, o = live[k]["z"], live[k]["o"]

@@ -45,13 +45,11 @@ def tile_matchmatrix_pa_t_w4_kernel(
         w1_sc = keep.tile([P, 2, K0], U8, align_bytes=64)
         w2 = keep.tile([P, 2 * K1], U8, align_bytes=64)
         w2_sc = keep.tile([P, K1], U8, align_bytes=64)
-        b_scales = keep.tile([P, P], U8, align_bytes=64)
         nc.vector.memset(w1_sc[:].rearrange("p g n -> p (g n)").bitcast(I32), 0)
-        nc.vector.memset(b_scales[:].bitcast(I32), 0)
         nc.vector.memset(w2_sc[:].bitcast(I32), 0)
-        nc.sync.dma_start(out=b_raw[:], in_=sent_b.rearrange("n j k -> (n j) k"))
         nc.sync.dma_start(out=a_bytes[:], in_=sent_a_bytes.rearrange("n (x h) k -> (n x) (h k)", h=H))
-        nc.scalar.dma_start(out=a_scale[:], in_=sent_a_scale.rearrange("x y (p t) -> p (x y t)", t=4))
+        nc.sync.dma_start(out=b_raw[:], in_=sent_b.rearrange("n j k -> (n j) k"))
+        nc.sync.dma_start(out=a_scale[:], in_=sent_a_scale.rearrange("x y (p t) -> p (x y t)", t=4))
         nc.sync.dma_start(out=w1[:].bitcast(I32), in_=w1_words.rearrange("g p n -> p g n").bitcast(I32))
         for q in range(4):
             nc.sync.dma_start(
@@ -85,13 +83,29 @@ def tile_matchmatrix_pa_t_w4_kernel(
                 nc.tensor.transpose(xt[:, u, :], words[:, u : 2 * P : 2], ident[:])
             return xt
 
-        a_raw = keep.tile([P, H * D], BF16, align_bytes=64)
-        b_grouped = keep.tile([P, P * 4], BF16, align_bytes=64)
-        b_codes = keep.tile([P, P], U32, align_bytes=64)
+        b_grouped = keep.tile([P, R * P * 4], BF16, align_bytes=64)
         rep_codes = keep.tile([P, R * P], U32, align_bytes=64)
         rep_scales = keep.tile([P, R * P], U8, align_bytes=64)
         a_part = [keep.tile([P, 4, P], F32, name=f"a_part{h}") for h in range(H)]
         b_part = [keep.tile([P, 4, P], F32, name=f"b_part{r}") for r in range(R)]
+
+        def widen(h):
+            a_raw = keep.tile([P, D], BF16, align_bytes=64, name=f"a_raw{h}")
+            nc.vector.tensor_copy(out=a_raw[:], in_=a_bytes[:, h * D : (h + 1) * D].bitcast(FP8))
+            return a_raw
+
+        def group_b(xt, r):
+            nc.scalar.copy(
+                out=b_grouped[:, r * D : (r + 1) * D].bitcast(F32).rearrange("p (n z w u) -> p n z w u", n=NB, z=Z, u=2),
+                in_=xt[:].rearrange("p u (n w r) -> p r n w u", n=NB, r=R)[:, r].unsqueeze(2).to_broadcast([P, NB, Z, W, 2]),
+            )
+
+        def quantize_b(r0, r1):
+            nc.vector.quantize_mx(
+                out=rep_codes[:, r0 * P : r1 * P].bitcast(FP8X4),
+                scales=rep_scales[:, r0 * P : r1 * P],
+                in_=b_grouped[:, r0 * D : r1 * D],
+            )
 
         def scale_a(h, xt):
             a_grouped = keep.tile([P, P, 2, 2], BF16, align_bytes=64, name=f"a_grouped{h}")
@@ -132,7 +146,7 @@ def tile_matchmatrix_pa_t_w4_kernel(
                 op=ALU.add,
             )
 
-        def b_layer(r):
+        def b_product(r):
             pb = xps.tile([P, K0], F32, name="pb", tag="x")
             cols = slice(r * P, (r + 1) * P)
             nc.tensor.matmul_mx(
@@ -144,13 +158,19 @@ def tile_matchmatrix_pa_t_w4_kernel(
                 start=True,
                 stop=True,
             )
-            nc.scalar.copy(out=b_part[r][:], in_=pb[:].rearrange("q (m t) -> q t m", t=4))
+            return pb
+
+        def b_rows(r, pb, engine):
+            if engine == "scalar":
+                nc.scalar.copy(out=b_part[r][:], in_=pb[:].rearrange("q (m t) -> q t m", t=4))
+            else:
+                nc.vector.tensor_copy(out=b_part[r][:], in_=pb[:].rearrange("q (m t) -> q t m", t=4))
 
         shift_order = [s for s in range(W) if s % (W // 2)] + [W // 2, 0]
         quads = [(h, s) for h in range(H) for s in shift_order]
         last = len(quads)
         units = [[0]] + [[q, q + 1] for q in range(1, last - 3, 2)] + [[q] for q in range(last - 3, last)]
-        twice = [0, 2, 3] + [R] * (len(units) - 3)
+        twice = [0,0,2] + [R] * (len(units) - 7) + [5,4,4,4]
         live = {}
 
         def sums(k, b):
@@ -159,8 +179,8 @@ def tile_matchmatrix_pa_t_w4_kernel(
             if b == 0:
                 live[k] = {"hidden": work.tile([P, 2 * R, P, 4], BF16, name="hidden", tag="hidden", align_bytes=64, bufs=3)}
                 if twice[k] > 0:
-                    live[k]["pair"] = work.tile([P, R, P, 4], BF16, name="pair", tag="pair", bufs=2)
-                    live[k]["small"] = work.tile([P, R, P, 4], BF16, name="small", tag="small", bufs=2)
+                    live[k]["pair"] = work.tile([P, twice[k], P, 4], BF16, name="pair", tag="pair", bufs=2)
+                    live[k]["small"] = work.tile([P, twice[k], P, 4], BF16, name="small", tag="small", bufs=2)
             x = xps.tile([P, 4, P], F32, name="x", tag="x")
             for t in range(4):
                 nc.tensor.matmul(
@@ -188,6 +208,12 @@ def tile_matchmatrix_pa_t_w4_kernel(
             nc.vector.tensor_tensor(
                 out=live[k]["hidden"][:, b0:b1], in0=live[k]["pair"][:, b0:b1], in1=live[k]["small"][:, b0:b1], op=ALU.max
             )
+
+        def activate(k, b0, b1):
+            if b0 < twice[k]:
+                leaky_pair(k, b0, min(b1, twice[k]))
+            for b in range(max(b0, twice[k]), b1):
+                leaky(k, b)
 
         def quantize(k, b0, b1):
             if b0 == 0:
@@ -218,7 +244,7 @@ def tile_matchmatrix_pa_t_w4_kernel(
         def add_bias(k, b0, b1):
             if b0 == 0:
                 live[k]["z"] = work.tile([P, 2 * R, K1], F32, name="z", tag="z", bufs=2)
-                live[k]["o"] = work.tile([P, 2 * R, K1], F32, name="o", tag="o", bufs=4)
+                live[k]["o"] = work.tile([P, 2 * R, K1], F32, name="o", tag="o", bufs=len(units))
             nc.vector.tensor_tensor(
                 out=live[k]["z"][:, b0:b1],
                 in0=live[k]["y", b0][:, : b1 - b0],
@@ -251,48 +277,43 @@ def tile_matchmatrix_pa_t_w4_kernel(
                 end = min(b + R, b1)
                 store(units[k][b // R], o[:, b:end], b % R, b % R + end - b)
 
+        a_raw0 = widen(0)
+        xt_a0 = turn(a_raw0[:])
         xt_b = turn(b_raw[:])
-        nc.vector.tensor_copy(out=a_raw[:], in_=a_bytes[:].bitcast(FP8))
-        xt_a = [turn(a_raw[:, h * D : (h + 1) * D]) for h in range(H)]
-        nc.scalar.copy(
-            out=b_grouped[:].bitcast(F32).rearrange("p (r c u) -> p r c u", r=R, u=2),
-            in_=xt_b[:].rearrange("p u (c r) -> p r c u", r=R),
-        )
-        nc.vector.quantize_mx(out=b_codes[:].bitcast(FP8X4), scales=b_scales[:], in_=b_grouped[:])
-        grouped0 = scale_a(0, xt_a[0])
-        nc.vector.tensor_copy(
-            out=rep_codes[:].bitcast(I32).rearrange("p (g z w) -> p g z w", z=Z, w=W),
-            in_=b_codes[:].bitcast(I32).rearrange("p (g w) -> p g w", w=W).unsqueeze(2).to_broadcast([P, R * NB, Z, W]),
-        )
-        nc.vector.tensor_copy(
-            out=rep_scales[:].bitcast(I32).rearrange("p (g z w) -> p g z w", z=Z, w=W // 4),
-            in_=b_scales[:]
-            .bitcast(I32)
-            .rearrange("p (g w) -> p g w", w=W // 4)
-            .unsqueeze(2)
-            .to_broadcast([P, R * NB, Z, W // 4]),
-        )
+        a_raw1 = widen(1)
+        xt_a1 = turn(a_raw1[:])
+        grouped0 = scale_a(0, xt_a0)
+        for r in range(R):
+            group_b(xt_b, r)
+        quantize_b(0, 1)
         quantized0 = quantize_a(0, grouped0)
-        grouped1 = scale_a(1, xt_a[1])
-        b_layer(0)
+        quantize_b(1, 2)
+        grouped1 = scale_a(1, xt_a1)
+        pb0 = b_product(0)
         pa0 = a_product(*quantized0)
-        b_layer(1)
-        b_layer(2)
-        a_rows(0, pa0)
+        pb1 = b_product(1)
+        b_rows(0, pb0, "scalar")
+        quantize_b(2, R)
         quantized1 = quantize_a(1, grouped1)
-        b_layer(3)
+        a_rows(0, pa0)
+        pb2 = b_product(2)
+        pb3 = b_product(3)
+        b_rows(1, pb1, "scalar")
+        b_rows(2, pb2, "vector")
+        pa1 = a_product(*quantized1)
+        b_rows(3, pb3, "scalar")
         sums(0, 0)
-        a_rows(1, a_product(*quantized1))
+        a_rows(1, pa1)
 
         for k in range(len(units)):
             blocks = R * len(units[k])
             old = range(0, R * len(units[k - 2]), R) if k >= 2 else []
             for b in range(1 if k == 0 else 0, blocks):
                 sums(k, b)
-                if b == 1:
+                if b == (1 if blocks > R else blocks - 1):
                     for b0 in old:
                         second_layer(k - 2, b0, b0 + R)
-            if k >= 2:
+            if k >= 1 and twice[k - 1] > 0:
                 leaky_pair(k - 1, 0, twice[k - 1])
             for b0 in old:
                 add_bias(k - 2, b0, b0 + R)
@@ -300,18 +321,19 @@ def tile_matchmatrix_pa_t_w4_kernel(
                 quantize(k - 1, 0, R * len(units[k - 1]))
             if k >= 2:
                 finish(k - 2, 0, R * len(units[k - 2]))
-            for b in range(twice[k], blocks):
-                leaky(k, b)
+            if k < len(units) - 1:
+                for b in range(twice[k], blocks):
+                    leaky(k, b)
 
         end = len(units) - 1
         half = R // 2
         second_layer(end - 1, 0, R)
-        leaky_pair(end, 0, half)
+        activate(end, 0, half)
         add_bias(end - 1, 0, R)
         quantize(end, 0, half)
         second_layer(end, 0, half)
         finish(end - 1, 0, R)
-        leaky_pair(end, half, R)
+        activate(end, half, R)
         add_bias(end, 0, half)
         quantize(end, half, R)
         second_layer(end, half, R)

@@ -13,6 +13,7 @@ FP8X4 = mybir.dt.float8_e4m3fn_x4
 FP4X4 = mybir.dt.float4_e2m1fn_x4
 ALU = mybir.AluOpType
 COPY = mybir.ActivationFunctionType.Copy
+RELU = mybir.ActivationFunctionType.Relu
 
 P = 128
 NB, NI, NJ, D, K0, K1 = 2, 128, 64, 512, 512, 128
@@ -170,14 +171,15 @@ def tile_matchmatrix_pa_t_w4_kernel(
         quads = [(h, s) for h in range(H) for s in shift_order]
         last = len(quads)
         units = [[0]] + [[q, q + 1] for q in range(1, last - 3, 2)] + [[q] for q in range(last - 3, last)]
-        twice = [0,0,2] + [R] * (len(units) - 7) + [5,4,4,4]
+        twice = [0,0,1] + [1 + k % 2 for k in range(len(units) - 7)] + [2,4,4,4]
         live = {}
+        ring = [keep.tile([P, 2 * R * P * 4], BF16, align_bytes=64, name=f"ring{i}") for i in range(4)]
 
         def sums(k, b):
             h, s = quads[units[k][b // R]]
             r = b % R
             if b == 0:
-                live[k] = {"hidden": work.tile([P, 2 * R, P, 4], BF16, name="hidden", tag="hidden", align_bytes=64, bufs=3)}
+                live[k] = {"hidden": ring[k % 4][:].rearrange("m (b c t) -> m b c t", c=P, t=4)}
                 if twice[k] > 0:
                     live[k]["pair"] = work.tile([P, twice[k], P, 4], BF16, name="pair", tag="pair", bufs=2)
                     live[k]["small"] = work.tile([P, twice[k], P, 4], BF16, name="small", tag="small", bufs=2)
@@ -243,8 +245,7 @@ def tile_matchmatrix_pa_t_w4_kernel(
 
         def add_bias(k, b0, b1):
             if b0 == 0:
-                live[k]["z"] = work.tile([P, 2 * R, K1], F32, name="z", tag="z", bufs=2)
-                live[k]["o"] = work.tile([P, 2 * R, K1], F32, name="o", tag="o", bufs=len(units))
+                live[k]["z"] = work.tile([P, 2 * R, K1], F32, name="z", tag="z", bufs=3)
             nc.vector.tensor_tensor(
                 out=live[k]["z"][:, b0:b1],
                 in0=live[k]["y", b0][:, : b1 - b0],
@@ -268,7 +269,23 @@ def tile_matchmatrix_pa_t_w4_kernel(
                     in_=o[w0 * M : (w0 + nw) * M].rearrange("c r k -> c (r k)"),
                 )
 
+        def lift(k):
+            blocks = R * len(units[k])
+            live[k]["lift"] = work.tile([P, 2 * R, K1], F32, name="lift", tag="lift", bufs=3)
+            nc.scalar.activation(out=live[k]["lift"][:, :blocks], in_=live[k]["z"][:, :blocks], func=RELU, scale=SLOPE - 1.0)
+
+        def join(k):
+            blocks = R * len(units[k])
+            o = ring[(k + 2) % 4][:].bitcast(F32).rearrange("c (b k) -> c b k", k=K1)
+            nc.gpsimd.tensor_tensor(
+                out=o[:, :blocks], in0=live[k]["z"][:, :blocks], in1=live[k]["lift"][:, :blocks], op=ALU.add
+            )
+            for b in range(0, blocks, R):
+                store(units[k][b // R], o[:, b : b + R], 0, R)
+
         def finish(k, b0, b1):
+            if b0 == 0:
+                live[k]["o"] = work.tile([P, 2 * R, K1], F32, name="o", tag="o", bufs=5)
             z, o = live[k]["z"], live[k]["o"]
             nc.vector.scalar_tensor_tensor(
                 out=o[:, b0:b1], in0=z[:, b0:b1], scalar=SLOPE, in1=z[:, b0:b1], op0=ALU.mult, op1=ALU.max
@@ -305,21 +322,36 @@ def tile_matchmatrix_pa_t_w4_kernel(
         sums(0, 0)
         a_rows(1, pa1)
 
+        closing = len(units) - 3
+        joined = len(units) - 6
         for k in range(len(units)):
             blocks = R * len(units[k])
-            old = range(0, R * len(units[k - 2]), R) if k >= 2 else []
-            for b in range(1 if k == 0 else 0, blocks):
+            early = min(blocks, 6 + 1)
+            for b in range(1 if k == 0 else 0, early):
                 sums(k, b)
-                if b == (1 if blocks > R else blocks - 1):
-                    for b0 in old:
-                        second_layer(k - 2, b0, b0 + R)
+                if b == 0 and 3 <= k < joined + 3:
+                    lift(k - 3)
+            old = range(0, R * len(units[k - 2]), R) if k >= 2 else []
+            ahead = 1 if k <= closing else 0
+            if k > closing:
+                for b0 in old:
+                    second_layer(k - 2, b0, b0 + R)
+            for b0 in old[:ahead]:
+                add_bias(k - 2, b0, b0 + R)
             if k >= 1 and twice[k - 1] > 0:
                 leaky_pair(k - 1, 0, twice[k - 1])
-            for b0 in old:
+            for b0 in old[ahead:]:
                 add_bias(k - 2, b0, b0 + R)
             if k >= 1:
                 quantize(k - 1, 0, R * len(units[k - 1]))
-            if k >= 2:
+            if 1 <= k < closing:
+                for b0 in range(0, R * len(units[k - 1]), R):
+                    second_layer(k - 1, b0, b0 + R)
+            for b in range(early, blocks):
+                sums(k, b)
+            if 3 <= k < joined + 3:
+                join(k - 3)
+            if k - 2 >= joined:
                 finish(k - 2, 0, R * len(units[k - 2]))
             if k < len(units) - 1:
                 for b in range(twice[k], blocks):

@@ -33,14 +33,14 @@ def tile_matchmatrix_pa_t_w4_kernel(
     with ExitStack() as ctx:
         keep = ctx.enter_context(tc.tile_pool(name="keep", bufs=1))
         work = ctx.enter_context(tc.tile_pool(name="work", bufs=4))
-        xps = ctx.enter_context(tc.psum_pool(name="xps", bufs=6))
-        yps = ctx.enter_context(tc.psum_pool(name="yps", bufs=2))
+        psum = ctx.enter_context(tc.psum_pool(name="psum", bufs=8))
         ctx.enter_context(tc.manual_schedule())
 
         b_raw = keep.tile([P, D], BF16, align_bytes=64)
         a_bytes = keep.tile([P, H * D], U8, align_bytes=64)
         a_scale = keep.tile([P, 4], F32)
-        b1_all = keep.tile([P, K0], BF16)
+        b1_cols = keep.tile([P, 4], BF16)
+        b1_all = keep.tile([P, 4, P], F32)
         b2_all = keep.tile([P, K1], BF16)
         w1 = keep.tile([P, 2, 2 * K0], U8, align_bytes=64)
         w1_sc = keep.tile([P, 2, K0], U8, align_bytes=64)
@@ -57,7 +57,7 @@ def tile_matchmatrix_pa_t_w4_kernel(
                 out=w1_sc[32 * q : 32 * q + 4, :, :].bitcast(I32),
                 in_=w1_scales[:, 4 * q : 4 * q + 4, :].rearrange("g q n -> q g n").bitcast(I32),
             )
-        nc.sync.dma_start(out=b1_all[:], in_=b1.partition_broadcast(P))
+        nc.sync.dma_start(out=b1_cols[:], in_=b1.rearrange("(m t) -> m t", t=4))
         nc.sync.dma_start(out=w2[:].bitcast(I32), in_=w2_words[0].bitcast(I32))
         for q in range(4):
             nc.sync.dma_start(
@@ -74,12 +74,15 @@ def tile_matchmatrix_pa_t_w4_kernel(
                 out=shifts[:, half * W : (half + 1) * W, :], in_=ident[:].rearrange("q (m w) -> q w m", w=W)
             )
 
+        ident_bf = keep.tile([P, P], BF16)
+        nc.vector.tensor_copy(out=ident_bf[:], in_=ident[:])
+
         def picks(s):
             return shifts[:].rearrange("q w m -> q (w m)")[:, s * M : s * M + P]
 
         def turn(raw):
             words = raw.bitcast(F32)
-            xt = xps.tile([P, 2, P], F32, name="xt", tag="x")
+            xt = psum.tile([P, 2, P], F32, name="xt", tag="x")
             for u in range(2):
                 nc.tensor.transpose(xt[:, u, :], words[:, u : 2 * P : 2], ident[:])
             return xt
@@ -127,7 +130,7 @@ def tile_matchmatrix_pa_t_w4_kernel(
             return a_codes, a_scales
 
         def a_product(a_codes, a_scales):
-            pa = yps.tile([P, K0], F32, name="pa", tag="y")
+            pa = psum.tile([P, K0], F32, name="pa", tag="x")
             nc.tensor.matmul_mx(
                 out=pa[:],
                 lhsT=a_codes[:].bitcast(FP8X4),
@@ -143,12 +146,12 @@ def tile_matchmatrix_pa_t_w4_kernel(
             nc.vector.tensor_tensor(
                 out=a_part[h][:],
                 in0=pa[:].rearrange("i (m t) -> i t m", t=4),
-                in1=b1_all[:].rearrange("i (m t) -> i t m", t=4),
+                in1=b1_all[:],
                 op=ALU.add,
             )
 
         def b_product(r):
-            pb = xps.tile([P, K0], F32, name="pb", tag="x")
+            pb = psum.tile([P, K0], F32, name="pb", tag="x")
             cols = slice(r * P, (r + 1) * P)
             nc.tensor.matmul_mx(
                 out=pb[:],
@@ -170,10 +173,12 @@ def tile_matchmatrix_pa_t_w4_kernel(
         shift_order = [s for s in range(W) if s % (W // 2)] + [W // 2, 0]
         quads = [(h, s) for h in range(H) for s in shift_order]
         last = len(quads)
-        units = [[0]] + [[q, q + 1] for q in range(1, last - 3, 2)] + [[q] for q in range(last - 3, last)]
+        sizes = [1] + [2] * 14 + [1] * 3
+        units = [list(range(sum(sizes[:k]), sum(sizes[: k + 1]))) for k in range(len(sizes))]
+        most = R * max(sizes)
         twice = [0,0,1] + [1 + k % 2 for k in range(len(units) - 7)] + [2,4,4,4]
         live = {}
-        ring = [keep.tile([P, 2 * R * P * 4], BF16, align_bytes=64, name=f"ring{i}") for i in range(4)]
+        ring = [keep.tile([P, most * P * 4], BF16, align_bytes=64, name=f"ring{i}") for i in range(4)]
 
         def sums(k, b):
             h, s = quads[units[k][b // R]]
@@ -183,7 +188,7 @@ def tile_matchmatrix_pa_t_w4_kernel(
                 if twice[k] > 0:
                     live[k]["pair"] = work.tile([P, twice[k], P, 4], BF16, name="pair", tag="pair", bufs=2)
                     live[k]["small"] = work.tile([P, twice[k], P, 4], BF16, name="small", tag="small", bufs=2)
-            x = xps.tile([P, 4, P], F32, name="x", tag="x")
+            x = psum.tile([P, 4, P], F32, name="x", tag="x")
             for t in range(4):
                 nc.tensor.matmul(
                     x[:, t, :], lhsT=a_part[h][:, t, :], rhs=picks(0), is_transpose=True, start=True, stop=False
@@ -218,9 +223,9 @@ def tile_matchmatrix_pa_t_w4_kernel(
                 leaky(k, b)
 
         def quantize(k, b0, b1):
-            if b0 == 0:
-                live[k]["codes"] = work.tile([P, 2 * R * P], U32, name="codes", tag="codes", align_bytes=64, bufs=3)
-                live[k]["scales"] = work.tile([P, 2 * R * P], U8, name="scales", tag="scales", align_bytes=64, bufs=3)
+            if "codes" not in live[k]:
+                live[k]["codes"] = work.tile([P, most * P], U32, name="codes", tag="codes", align_bytes=64, bufs=2)
+                live[k]["scales"] = work.tile([P, most * P], U8, name="scales", tag="scales", align_bytes=64, bufs=2)
             cols = slice(b0 * P, b1 * P)
             nc.vector.quantize_mx(
                 out=live[k]["codes"][:, cols].bitcast(FP8X4),
@@ -229,7 +234,7 @@ def tile_matchmatrix_pa_t_w4_kernel(
             )
 
         def second_layer(k, b0, b1):
-            y = yps.tile([P, R, K1], F32, name="y", tag="y")
+            y = psum.tile([P, R, K1], F32, name="y", tag="x")
             for b in range(b0, b1):
                 cols = slice(b * P, (b + 1) * P)
                 nc.tensor.matmul_mx(
@@ -245,7 +250,7 @@ def tile_matchmatrix_pa_t_w4_kernel(
 
         def add_bias(k, b0, b1):
             if b0 == 0:
-                live[k]["z"] = work.tile([P, 2 * R, K1], F32, name="z", tag="z", bufs=3)
+                live[k]["z"] = work.tile([P, most, K1], F32, name="z", tag="z", bufs=3)
             nc.vector.tensor_tensor(
                 out=live[k]["z"][:, b0:b1],
                 in0=live[k]["y", b0][:, : b1 - b0],
@@ -271,12 +276,12 @@ def tile_matchmatrix_pa_t_w4_kernel(
 
         def lift(k):
             blocks = R * len(units[k])
-            live[k]["lift"] = work.tile([P, 2 * R, K1], F32, name="lift", tag="lift", bufs=3)
+            live[k]["lift"] = work.tile([P, most, K1], F32, name="lift", tag="lift", bufs=2)
             nc.scalar.activation(out=live[k]["lift"][:, :blocks], in_=live[k]["z"][:, :blocks], func=RELU, scale=SLOPE - 1.0)
 
         def join(k):
             blocks = R * len(units[k])
-            o = ring[(k + 2) % 4][:].bitcast(F32).rearrange("c (b k) -> c b k", k=K1)
+            o = ring[(k + 1) % 4][:].bitcast(F32).rearrange("c (b k) -> c b k", k=K1)
             nc.gpsimd.tensor_tensor(
                 out=o[:, :blocks], in0=live[k]["z"][:, :blocks], in1=live[k]["lift"][:, :blocks], op=ALU.add
             )
@@ -285,7 +290,7 @@ def tile_matchmatrix_pa_t_w4_kernel(
 
         def finish(k, b0, b1):
             if b0 == 0:
-                live[k]["o"] = work.tile([P, 2 * R, K1], F32, name="o", tag="o", bufs=5)
+                live[k]["o"] = work.tile([P, R * sizes[k], K1], F32, name="o", tag="o", bufs=6)
             z, o = live[k]["z"], live[k]["o"]
             nc.vector.scalar_tensor_tensor(
                 out=o[:, b0:b1], in0=z[:, b0:b1], scalar=SLOPE, in1=z[:, b0:b1], op0=ALU.mult, op1=ALU.max
@@ -299,9 +304,15 @@ def tile_matchmatrix_pa_t_w4_kernel(
         xt_b = turn(b_raw[:])
         a_raw1 = widen(1)
         xt_a1 = turn(a_raw1[:])
+        spread = psum.tile([P, 4, P], F32, name="spread", tag="x")
+        for t in range(4):
+            nc.tensor.matmul(
+                spread[:, t, :], lhsT=b1_cols[:, t : t + 1].to_broadcast([P, P]), rhs=ident_bf[:], start=True, stop=True
+            )
         grouped0 = scale_a(0, xt_a0)
         for r in range(R):
             group_b(xt_b, r)
+        nc.scalar.copy(out=b1_all[:], in_=spread[:])
         quantize_b(0, 1)
         quantized0 = quantize_a(0, grouped0)
         quantize_b(1, 2)
@@ -323,16 +334,14 @@ def tile_matchmatrix_pa_t_w4_kernel(
         a_rows(1, pa1)
 
         closing = len(units) - 3
-        joined = len(units) - 6
+        joined = len(units) - 5
         for k in range(len(units)):
             blocks = R * len(units[k])
-            early = min(blocks, 6 + 1)
+            early = min(blocks, 3 + 1)
             for b in range(1 if k == 0 else 0, early):
                 sums(k, b)
-                if b == 0 and 3 <= k < joined + 3:
-                    lift(k - 3)
             old = range(0, R * len(units[k - 2]), R) if k >= 2 else []
-            ahead = 1 if k <= closing else 0
+            ahead = (len(old) + 1) // 2 if k <= closing else 0
             if k > closing:
                 for b0 in old:
                     second_layer(k - 2, b0, b0 + R)
@@ -343,14 +352,16 @@ def tile_matchmatrix_pa_t_w4_kernel(
             for b0 in old[ahead:]:
                 add_bias(k - 2, b0, b0 + R)
             if k >= 1:
-                quantize(k - 1, 0, R * len(units[k - 1]))
+                for b0 in reversed(range(0, R * len(units[k - 1]), 2 * R)):
+                    quantize(k - 1, b0, min(b0 + 2 * R, R * len(units[k - 1])))
+            if 2 <= k < joined + 2:
+                lift(k - 2)
+                join(k - 2)
+            for b in range(early, blocks):
+                sums(k, b)
             if 1 <= k < closing:
                 for b0 in range(0, R * len(units[k - 1]), R):
                     second_layer(k - 1, b0, b0 + R)
-            for b in range(early, blocks):
-                sums(k, b)
-            if 3 <= k < joined + 3:
-                join(k - 3)
             if k - 2 >= joined:
                 finish(k - 2, 0, R * len(units[k - 2]))
             if k < len(units) - 1:

@@ -51,12 +51,12 @@ def tile_matchmatrix_pa_t_w4_kernel(
         nc.sync.dma_start(out=a_bytes[:], in_=sent_a_bytes.rearrange("n (x h) k -> (n x) (h k)", h=H))
         nc.sync.dma_start(out=b_raw[:], in_=sent_b.rearrange("n j k -> (n j) k"))
         nc.sync.dma_start(out=a_scale[:], in_=sent_a_scale.rearrange("x y (p t) -> p (x y t)", t=4))
-        nc.sync.dma_start(out=w1[:].bitcast(I32), in_=w1_words.rearrange("g p n -> p g n").bitcast(I32))
         for q in range(4):
             nc.sync.dma_start(
                 out=w1_sc[32 * q : 32 * q + 4, :, :].bitcast(I32),
                 in_=w1_scales[:, 4 * q : 4 * q + 4, :].rearrange("g q n -> q g n").bitcast(I32),
             )
+        nc.sync.dma_start(out=w1[:].bitcast(I32), in_=w1_words.rearrange("g p n -> p g n").bitcast(I32))
         nc.sync.dma_start(out=b1_cols[:], in_=b1.rearrange("(m t) -> m t", t=4))
         nc.sync.dma_start(out=w2[:].bitcast(I32), in_=w2_words[0].bitcast(I32))
         for q in range(4):
@@ -313,12 +313,12 @@ def tile_matchmatrix_pa_t_w4_kernel(
         for r in range(R):
             group_b(xt_b, r)
         nc.scalar.copy(out=b1_all[:], in_=spread[:])
-        quantize_b(0, 1)
         quantized0 = quantize_a(0, grouped0)
+        quantize_b(0, 1)
         quantize_b(1, 2)
         grouped1 = scale_a(1, xt_a1)
-        pb0 = b_product(0)
         pa0 = a_product(*quantized0)
+        pb0 = b_product(0)
         pb1 = b_product(1)
         b_rows(0, pb0, "scalar")
         quantize_b(2, R)

@@ -176,7 +176,7 @@ def tile_matchmatrix_pa_t_w4_kernel(
         sizes = [1] + [2] * 14 + [1] * 3
         units = [list(range(sum(sizes[:k]), sum(sizes[: k + 1]))) for k in range(len(sizes))]
         most = R * max(sizes)
-        twice = [0,0,1] + [1 + k % 2 for k in range(len(units) - 7)] + [2,4,4,4]
+        twice = [0,0,1] + [1 + k % 2 for k in range(len(units) - 7)] + [2,0,4,4]
         live = {}
         ring = [keep.tile([P, most * P * 4], BF16, align_bytes=64, name=f"ring{i}") for i in range(4)]
 
@@ -334,7 +334,7 @@ def tile_matchmatrix_pa_t_w4_kernel(
         a_rows(1, pa1)
 
         closing = len(units) - 3
-        joined = len(units) - 5
+        joined = len(units) - 4
         for k in range(len(units)):
             blocks = R * len(units[k])
             early = min(blocks, 3 + 1)

@@ -176,7 +176,8 @@ def tile_matchmatrix_pa_t_w4_kernel(
         sizes = [1] + [2] * 14 + [1] * 3
         units = [list(range(sum(sizes[:k]), sum(sizes[: k + 1]))) for k in range(len(sizes))]
         most = R * max(sizes)
-        twice = [0,0,1] + [1 + k % 2 for k in range(len(units) - 7)] + [2,0,4,4]
+        twice = [0, 0, 1] + [1] * (len(units) - 7) + [2, 0, 4, 4]
+        on_gpsimd = len(units) - 4
         live = {}
         ring = [keep.tile([P, most * P * 4], BF16, align_bytes=64, name=f"ring{i}") for i in range(4)]
 
@@ -201,6 +202,9 @@ def tile_matchmatrix_pa_t_w4_kernel(
                 first = work.tile([P, P, 4], BF16, name="first", tag="first", bufs=8)
                 nc.scalar.copy(out=first[:], in_=view)
                 live[k][b] = (view, first)
+            elif k < on_gpsimd:
+                nc.scalar.activation(out=live[k]["pair"][:, b], in_=view, func=RELU)
+                nc.scalar.activation(out=live[k]["small"][:, b], in_=view, func=RELU, scale=-SLOPE)
             else:
                 nc.scalar.copy(out=live[k]["pair"][:, b], in_=view)
                 nc.scalar.activation(out=live[k]["small"][:, b], in_=view, func=COPY, scale=SLOPE)
@@ -214,6 +218,12 @@ def tile_matchmatrix_pa_t_w4_kernel(
         def leaky_pair(k, b0, b1):
             nc.vector.tensor_tensor(
                 out=live[k]["hidden"][:, b0:b1], in0=live[k]["pair"][:, b0:b1], in1=live[k]["small"][:, b0:b1], op=ALU.max
+            )
+
+        def leaky_parts(k):
+            n = twice[k]
+            nc.gpsimd.tensor_tensor(
+                out=live[k]["hidden"][:, :n], in0=live[k]["pair"][:, :n], in1=live[k]["small"][:, :n], op=ALU.subtract
             )
 
         def activate(k, b0, b1):
@@ -347,7 +357,7 @@ def tile_matchmatrix_pa_t_w4_kernel(
                     second_layer(k - 2, b0, b0 + R)
             for b0 in old[:ahead]:
                 add_bias(k - 2, b0, b0 + R)
-            if k >= 1 and twice[k - 1] > 0:
+            if k - 1 >= on_gpsimd and twice[k - 1] > 0:
                 leaky_pair(k - 1, 0, twice[k - 1])
             for b0 in old[ahead:]:
                 add_bias(k - 2, b0, b0 + R)
@@ -357,6 +367,8 @@ def tile_matchmatrix_pa_t_w4_kernel(
             if 2 <= k < joined + 2:
                 lift(k - 2)
                 join(k - 2)
+            if k < on_gpsimd and twice[k] > 0:
+                leaky_parts(k)
             for b in range(early, blocks):
                 sums(k, b)
             if 1 <= k < closing:

@@ -24,6 +24,7 @@ W = NJ // R
 Z = P // (NB * W)
 M = NB * Z
 H = NB * NI // P
+RING = 6
 
 
 def tile_matchmatrix_pa_t_w4_kernel(
@@ -32,7 +33,7 @@ def tile_matchmatrix_pa_t_w4_kernel(
     nc = tc.nc
     with ExitStack() as ctx:
         keep = ctx.enter_context(tc.tile_pool(name="keep", bufs=1))
-        work = ctx.enter_context(tc.tile_pool(name="work", bufs=4))
+        work = ctx.enter_context(tc.tile_pool(name="work", bufs=2))
         psum = ctx.enter_context(tc.psum_pool(name="psum", bufs=8))
         ctx.enter_context(tc.manual_schedule())
 
@@ -73,7 +74,6 @@ def tile_matchmatrix_pa_t_w4_kernel(
             nc.vector.tensor_copy(
                 out=shifts[:, half * W : (half + 1) * W, :], in_=ident[:].rearrange("q (m w) -> q w m", w=W)
             )
-
         ident_bf = keep.tile([P, P], BF16)
         nc.vector.tensor_copy(out=ident_bf[:], in_=ident[:])
 
@@ -82,14 +82,14 @@ def tile_matchmatrix_pa_t_w4_kernel(
 
         def turn(raw):
             words = raw.bitcast(F32)
-            xt = psum.tile([P, 2, P], F32, name="xt", tag="x")
+            xt = psum.tile([P, 2, P], F32, name="xt", tag="bank")
             for u in range(2):
                 nc.tensor.transpose(xt[:, u, :], words[:, u : 2 * P : 2], ident[:])
             return xt
 
         b_grouped = keep.tile([P, R * P * 4], BF16, align_bytes=64)
-        rep_codes = keep.tile([P, R * P], U32, align_bytes=64)
-        rep_scales = keep.tile([P, R * P], U8, align_bytes=64)
+        b_codes = keep.tile([P, R * P], U32, align_bytes=64)
+        b_scales = keep.tile([P, R * P], U8, align_bytes=64)
         a_part = [keep.tile([P, 4, P], F32, name=f"a_part{h}") for h in range(H)]
         b_part = [keep.tile([P, 4, P], F32, name=f"b_part{r}") for r in range(R)]
 
@@ -106,8 +106,8 @@ def tile_matchmatrix_pa_t_w4_kernel(
 
         def quantize_b(r0, r1):
             nc.vector.quantize_mx(
-                out=rep_codes[:, r0 * P : r1 * P].bitcast(FP8X4),
-                scales=rep_scales[:, r0 * P : r1 * P],
+                out=b_codes[:, r0 * P : r1 * P].bitcast(FP8X4),
+                scales=b_scales[:, r0 * P : r1 * P],
                 in_=b_grouped[:, r0 * D : r1 * D],
             )
 
@@ -127,180 +127,153 @@ def tile_matchmatrix_pa_t_w4_kernel(
             nc.vector.quantize_mx(
                 out=a_codes[:].bitcast(FP8X4), scales=a_scales[:], in_=a_grouped[:].rearrange("p c u e -> p (c u e)")
             )
-            return a_codes, a_scales
+            return a_codes[:], a_scales[:]
 
-        def a_product(a_codes, a_scales):
-            pa = psum.tile([P, K0], F32, name="pa", tag="x")
+        def first_layer(codes, scales, g):
+            bank = psum.tile([P, K0], F32, name="product", tag="bank")
             nc.tensor.matmul_mx(
-                out=pa[:],
-                lhsT=a_codes[:].bitcast(FP8X4),
-                lhsT_scale=a_scales[:],
-                rhs=w1[:, 0, :].bitcast(FP4X4),
-                rhs_scale=w1_sc[:, 0, :],
+                out=bank[:],
+                lhsT=codes.bitcast(FP8X4),
+                lhsT_scale=scales,
+                rhs=w1[:, g, :].bitcast(FP4X4),
+                rhs_scale=w1_sc[:, g, :],
                 start=True,
                 stop=True,
             )
-            return pa
-
-        def a_rows(h, pa):
-            nc.vector.tensor_tensor(
-                out=a_part[h][:],
-                in0=pa[:].rearrange("i (m t) -> i t m", t=4),
-                in1=b1_all[:],
-                op=ALU.add,
-            )
+            return bank[:].rearrange("q (m t) -> q t m", t=4)
 
         def b_product(r):
-            pb = psum.tile([P, K0], F32, name="pb", tag="x")
-            cols = slice(r * P, (r + 1) * P)
-            nc.tensor.matmul_mx(
-                out=pb[:],
-                lhsT=rep_codes[:, cols].bitcast(FP8X4),
-                lhsT_scale=rep_scales[:, cols],
-                rhs=w1[:, 1, :].bitcast(FP4X4),
-                rhs_scale=w1_sc[:, 1, :],
-                start=True,
-                stop=True,
-            )
-            return pb
+            return first_layer(b_codes[:, r * P : (r + 1) * P], b_scales[:, r * P : (r + 1) * P], 1)
 
-        def b_rows(r, pb, engine):
-            if engine == "scalar":
-                nc.scalar.copy(out=b_part[r][:], in_=pb[:].rearrange("q (m t) -> q t m", t=4))
-            else:
-                nc.vector.tensor_copy(out=b_part[r][:], in_=pb[:].rearrange("q (m t) -> q t m", t=4))
+        def a_rows(h, product):
+            nc.vector.tensor_tensor(out=a_part[h][:], in0=product, in1=b1_all[:], op=ALU.add)
 
-        shift_order = [s for s in range(W) if s % (W // 2)] + [W // 2, 0]
-        quads = [(h, s) for h in range(H) for s in shift_order]
-        last = len(quads)
+        quads = [(h, s) for s in list(range(1, W)) + [0] for h in range(H)]
         sizes = [1] + [2] * 14 + [1] * 3
         units = [list(range(sum(sizes[:k]), sum(sizes[: k + 1]))) for k in range(len(sizes))]
         most = R * max(sizes)
-        twice = [0, 0, 1] + [1] * (len(units) - 7) + [2, 0, 4, 4]
-        on_gpsimd = len(units) - 4
-        live = {}
-        ring = [keep.tile([P, most * P * 4], BF16, align_bytes=64, name=f"ring{i}") for i in range(4)]
+        last = len(units) - 1
+        steady = range(2, last - 3)
+        twice = [1 if k in steady else R if k >= last - 1 else 0 for k in range(len(units))]
+        direct = range(3, last - 4, 3)
+        live = [{} for k in units]
+        ring = [keep.tile([P, most * P * 4], BF16, align_bytes=64, name=f"ring{i}") for i in range(RING)]
+
+        def blocks(k):
+            return R * len(units[k])
+
+        def hidden(k):
+            return ring[k % RING][:].rearrange("m (b c t) -> m b c t", c=P, t=4)
 
         def sums(k, b):
             h, s = quads[units[k][b // R]]
-            r = b % R
-            if b == 0:
-                live[k] = {"hidden": ring[k % 4][:].rearrange("m (b c t) -> m b c t", c=P, t=4)}
-                if twice[k] > 0:
-                    live[k]["pair"] = work.tile([P, twice[k], P, 4], BF16, name="pair", tag="pair", bufs=2)
-                    live[k]["small"] = work.tile([P, twice[k], P, 4], BF16, name="small", tag="small", bufs=2)
-            x = psum.tile([P, 4, P], F32, name="x", tag="x")
+            x = psum.tile([P, 4, P], F32, name="x", tag="bank")
             for t in range(4):
                 nc.tensor.matmul(
                     x[:, t, :], lhsT=a_part[h][:, t, :], rhs=picks(0), is_transpose=True, start=True, stop=False
                 )
                 nc.tensor.matmul(
-                    x[:, t, :], lhsT=b_part[r][:, t, :], rhs=picks(s), is_transpose=True, start=False, stop=True
+                    x[:, t, :], lhsT=b_part[b % R][:, t, :], rhs=picks(s), is_transpose=True, start=False, stop=True
                 )
             view = x[:].rearrange("m t c -> m c t")
             if b >= twice[k]:
                 first = work.tile([P, P, 4], BF16, name="first", tag="first", bufs=8)
                 nc.scalar.copy(out=first[:], in_=view)
                 live[k][b] = (view, first)
-            elif k < on_gpsimd:
-                nc.scalar.activation(out=live[k]["pair"][:, b], in_=view, func=RELU)
-                nc.scalar.activation(out=live[k]["small"][:, b], in_=view, func=RELU, scale=-SLOPE)
+                return
+            if b == 0:
+                live[k]["one"] = work.tile([P, twice[k], P, 4], BF16, name="one", tag="one")
+                live[k]["other"] = work.tile([P, twice[k], P, 4], BF16, name="other", tag="other")
+            if k in steady:
+                nc.scalar.activation(out=live[k]["one"][:, b], in_=view, func=RELU)
+                nc.scalar.activation(out=live[k]["other"][:, b], in_=view, func=RELU, scale=-SLOPE)
             else:
-                nc.scalar.copy(out=live[k]["pair"][:, b], in_=view)
-                nc.scalar.activation(out=live[k]["small"][:, b], in_=view, func=COPY, scale=SLOPE)
+                nc.scalar.copy(out=live[k]["one"][:, b], in_=view)
+                nc.scalar.activation(out=live[k]["other"][:, b], in_=view, func=COPY, scale=SLOPE)
 
         def leaky(k, b):
             view, first = live[k][b]
             nc.vector.scalar_tensor_tensor(
-                out=live[k]["hidden"][:, b], in0=view, scalar=SLOPE, in1=first[:], op0=ALU.mult, op1=ALU.max
+                out=hidden(k)[:, b], in0=view, scalar=SLOPE, in1=first[:], op0=ALU.mult, op1=ALU.max
             )
 
-        def leaky_pair(k, b0, b1):
+        def leaky_max(k, b0, b1):
             nc.vector.tensor_tensor(
-                out=live[k]["hidden"][:, b0:b1], in0=live[k]["pair"][:, b0:b1], in1=live[k]["small"][:, b0:b1], op=ALU.max
+                out=hidden(k)[:, b0:b1], in0=live[k]["one"][:, b0:b1], in1=live[k]["other"][:, b0:b1], op=ALU.max
             )
 
         def leaky_parts(k):
-            n = twice[k]
             nc.gpsimd.tensor_tensor(
-                out=live[k]["hidden"][:, :n], in0=live[k]["pair"][:, :n], in1=live[k]["small"][:, :n], op=ALU.subtract
+                out=hidden(k)[:, : twice[k]], in0=live[k]["one"][:], in1=live[k]["other"][:], op=ALU.subtract
             )
 
-        def activate(k, b0, b1):
-            if b0 < twice[k]:
-                leaky_pair(k, b0, min(b1, twice[k]))
-            for b in range(max(b0, twice[k]), b1):
-                leaky(k, b)
-
         def quantize(k, b0, b1):
-            if "codes" not in live[k]:
-                live[k]["codes"] = work.tile([P, most * P], U32, name="codes", tag="codes", align_bytes=64, bufs=2)
-                live[k]["scales"] = work.tile([P, most * P], U8, name="scales", tag="scales", align_bytes=64, bufs=2)
+            if b0 == 0:
+                live[k]["codes"] = work.tile([P, most * P], U32, name="codes", tag="codes", align_bytes=64)
+                live[k]["scales"] = work.tile([P, most * P], U8, name="scales", tag="scales", align_bytes=64)
             cols = slice(b0 * P, b1 * P)
             nc.vector.quantize_mx(
                 out=live[k]["codes"][:, cols].bitcast(FP8X4),
                 scales=live[k]["scales"][:, cols],
-                in_=live[k]["hidden"][:, b0:b1].rearrange("m b c t -> m (b c t)"),
+                in_=hidden(k)[:, b0:b1].rearrange("m b c t -> m (b c t)"),
             )
 
         def second_layer(k, b0, b1):
-            y = psum.tile([P, R, K1], F32, name="y", tag="x")
-            for b in range(b0, b1):
-                cols = slice(b * P, (b + 1) * P)
-                nc.tensor.matmul_mx(
-                    out=y[:, b - b0, :],
-                    lhsT=live[k]["codes"][:, cols].bitcast(FP8X4),
-                    lhsT_scale=live[k]["scales"][:, cols],
-                    rhs=w2[:].bitcast(FP4X4),
-                    rhs_scale=w2_sc[:],
-                    start=True,
-                    stop=True,
-                )
-            live[k]["y", b0] = y
+            for first in range(b0, b1, R):
+                y = psum.tile([P, R, K1], F32, name="y", tag="bank")
+                for b in range(first, min(first + R, b1)):
+                    cols = slice(b * P, (b + 1) * P)
+                    nc.tensor.matmul_mx(
+                        out=y[:, b - first, :],
+                        lhsT=live[k]["codes"][:, cols].bitcast(FP8X4),
+                        lhsT_scale=live[k]["scales"][:, cols],
+                        rhs=w2[:].bitcast(FP4X4),
+                        rhs_scale=w2_sc[:],
+                        start=True,
+                        stop=True,
+                    )
+                live[k]["y", first] = y
 
         def add_bias(k, b0, b1):
             if b0 == 0:
                 live[k]["z"] = work.tile([P, most, K1], F32, name="z", tag="z", bufs=3)
-            nc.vector.tensor_tensor(
-                out=live[k]["z"][:, b0:b1],
-                in0=live[k]["y", b0][:, : b1 - b0],
-                in1=b2_all[:].unsqueeze(1).to_broadcast([P, b1 - b0, K1]),
-                op=ALU.add,
-            )
+            for first in range(b0, b1, R):
+                n = min(R, b1 - first)
+                nc.vector.tensor_tensor(
+                    out=live[k]["z"][:, first : first + n],
+                    in0=live[k]["y", first][:, :n],
+                    in1=b2_all[:].unsqueeze(1).to_broadcast([P, n, K1]),
+                    op=ALU.add,
+                )
 
-        rows = out.rearrange("n (z x) j k -> (n z) (x j k)", z=Z)
-        span = rows.shape[1]
-        step = H * NJ * K1 + R * K1
+        runs = out.rearrange("n (z x) (g r) k -> (n z) (x g) (r k)", z=Z, r=R)
+        step = H * W + 1
 
         def store(q, o, r0, r1):
             h, s = quads[q]
-            cut = W - s if s else W // 2
-            for w0, nw in ((0, cut), (cut, W - cut)):
-                base = w0 * step + h * NJ * K1 + s * R * K1 - (NJ * K1 if w0 + s >= W else 0)
-                early = max(0, base + nw * step - span)
-                window = rows[:, base - early : base - early + nw * step].rearrange("m (w x) -> w m x", x=step)
+            for w0, w1 in ((0, W - s), (W - s, W)) if s else ((0, W),):
+                start = w0 * step + h * W + (w0 + s) % W - w0
                 nc.sync.dma_start(
-                    out=window[:, :, early + r0 * K1 : early + r1 * K1],
-                    in_=o[w0 * M : (w0 + nw) * M].rearrange("c r k -> c (r k)"),
+                    out=runs[:, start : start + (w1 - w0 - 1) * step + 1 : step, r0 * K1 : r1 * K1].rearrange("m w x -> w m x"),
+                    in_=o[w0 * M : w1 * M].rearrange("c r k -> c (r k)"),
                 )
 
         def lift(k):
-            blocks = R * len(units[k])
-            live[k]["lift"] = work.tile([P, most, K1], F32, name="lift", tag="lift", bufs=2)
-            nc.scalar.activation(out=live[k]["lift"][:, :blocks], in_=live[k]["z"][:, :blocks], func=RELU, scale=SLOPE - 1.0)
-
-        def join(k):
-            blocks = R * len(units[k])
-            o = ring[(k + 1) % 4][:].bitcast(F32).rearrange("c (b k) -> c b k", k=K1)
-            nc.gpsimd.tensor_tensor(
-                out=o[:, :blocks], in0=live[k]["z"][:, :blocks], in1=live[k]["lift"][:, :blocks], op=ALU.add
+            live[k]["lift"] = work.tile([P, most, K1], F32, name="lift", tag="lift")
+            nc.scalar.activation(
+                out=live[k]["lift"][:, : blocks(k)], in_=live[k]["z"][:, : blocks(k)], func=RELU, scale=SLOPE - 1.0
             )
-            for b in range(0, blocks, R):
+
+        def join(k, after):
+            o = ring[after % RING][:].bitcast(F32).rearrange("c (b k) -> c b k", k=K1)
+            n = blocks(k)
+            nc.gpsimd.tensor_tensor(out=o[:, :n], in0=live[k]["z"][:, :n], in1=live[k]["lift"][:, :n], op=ALU.add)
+            for b in range(0, n, R):
                 store(units[k][b // R], o[:, b : b + R], 0, R)
 
         def finish(k, b0, b1):
             if b0 == 0:
-                live[k]["o"] = work.tile([P, R * sizes[k], K1], F32, name="o", tag="o", bufs=6)
+                live[k]["o"] = work.tile([P, blocks(k), K1], F32, name="o", tag="o", bufs=4)
             z, o = live[k]["z"], live[k]["o"]
             nc.vector.scalar_tensor_tensor(
                 out=o[:, b0:b1], in0=z[:, b0:b1], scalar=SLOPE, in1=z[:, b0:b1], op0=ALU.mult, op1=ALU.max
@@ -309,12 +282,51 @@ def tile_matchmatrix_pa_t_w4_kernel(
                 end = min(b + R, b1)
                 store(units[k][b // R], o[:, b:end], b % R, b % R + end - b)
 
+        a_small = keep.tile([P, P, 4], F32)
+        b_small = keep.tile([P, 2 * W * NB, 4], F32)
+
+        def turn_small():
+            xa = psum.tile([P, 4, P], F32, name="xa", tag="bank")
+            xb = psum.tile([P, 4, P], F32, name="xb", tag="bank")
+            for t in range(4):
+                nc.tensor.transpose(xa[:, t, :], a_part[0][:, t, :], picks(0))
+            for t in range(4):
+                nc.tensor.transpose(xb[:, t, :], b_part[R - 1][:, t, :], picks(0))
+            nc.scalar.activation(out=a_small[:], in_=xa[:].rearrange("m t c -> m c t"), func=COPY, scale=SLOPE)
+            nc.scalar.activation(
+                out=b_small[:].rearrange("m (d g) t -> m d g t", d=2),
+                in_=xb[:].rearrange("m t (g z) -> m z g t", z=Z)[:, 0].unsqueeze(1).to_broadcast([P, 2, W * NB, 4]),
+                func=COPY,
+                scale=SLOPE,
+            )
+
+        def direct_sum(k):
+            s = quads[units[k][-1]][1]
+            low = work.tile([P, P, 4], F32, name="low", tag="low", bufs=len(direct))
+            nc.gpsimd.tensor_tensor(
+                out=low[:].rearrange("m (g z) t -> m g z t", z=Z),
+                in0=a_small[:].rearrange("m (g z) t -> m g z t", z=Z),
+                in1=b_small[:, s * NB : (s + W) * NB, :].unsqueeze(2).to_broadcast([P, W * NB, Z, 4]),
+                op=ALU.add,
+            )
+            live[k]["low"] = low
+
+        def direct_half(k, half):
+            cols = slice(half * P // 2, (half + 1) * P // 2)
+            low = live[k]["low"][:, cols]
+            high = work.tile([P, P // 2, 4], F32, name="high", tag="high")
+            nc.scalar.activation(out=high[:], in_=low, func=RELU, scale=(1.0 - SLOPE) / SLOPE)
+            nc.gpsimd.tensor_tensor(out=hidden(k)[:, blocks(k) - 1, cols], in0=low, in1=high[:], op=ALU.add)
+
+        def summed(k):
+            return blocks(k) - (1 if k in direct else 0)
+
         a_raw0 = widen(0)
         xt_a0 = turn(a_raw0[:])
         xt_b = turn(b_raw[:])
         a_raw1 = widen(1)
         xt_a1 = turn(a_raw1[:])
-        spread = psum.tile([P, 4, P], F32, name="spread", tag="x")
+        spread = psum.tile([P, 4, P], F32, name="spread", tag="bank")
         for t in range(4):
             nc.tensor.matmul(
                 spread[:, t, :], lhsT=b1_cols[:, t : t + 1].to_broadcast([P, P]), rhs=ident_bf[:], start=True, stop=True
@@ -327,71 +339,89 @@ def tile_matchmatrix_pa_t_w4_kernel(
         quantize_b(0, 1)
         quantize_b(1, 2)
         grouped1 = scale_a(1, xt_a1)
-        pa0 = a_product(*quantized0)
+        pa0 = first_layer(*quantized0, 0)
         pb0 = b_product(0)
         pb1 = b_product(1)
-        b_rows(0, pb0, "scalar")
+        nc.scalar.copy(out=b_part[0][:], in_=pb0)
         quantize_b(2, R)
         quantized1 = quantize_a(1, grouped1)
         a_rows(0, pa0)
         pb2 = b_product(2)
         pb3 = b_product(3)
-        b_rows(1, pb1, "scalar")
-        b_rows(2, pb2, "vector")
-        pa1 = a_product(*quantized1)
-        b_rows(3, pb3, "scalar")
+        nc.scalar.copy(out=b_part[1][:], in_=pb1)
+        nc.vector.tensor_copy(out=b_part[2][:], in_=pb2)
+        pa1 = first_layer(*quantized1, 0)
+        nc.scalar.copy(out=b_part[3][:], in_=pb3)
         sums(0, 0)
         a_rows(1, pa1)
 
-        closing = len(units) - 3
-        joined = len(units) - 4
-        for k in range(len(units)):
-            blocks = R * len(units[k])
-            early = min(blocks, 3 + 1)
-            for b in range(1 if k == 0 else 0, early):
+        for k in range(last - 2):
+            for b in range(1 if k == 0 else 0, R):
                 sums(k, b)
-            old = range(0, R * len(units[k - 2]), R) if k >= 2 else []
-            ahead = (len(old) + 1) // 2 if k <= closing else 0
-            if k > closing:
-                for b0 in old:
-                    second_layer(k - 2, b0, b0 + R)
-            for b0 in old[:ahead]:
-                add_bias(k - 2, b0, b0 + R)
-            if k - 1 >= on_gpsimd and twice[k - 1] > 0:
-                leaky_pair(k - 1, 0, twice[k - 1])
-            for b0 in old[ahead:]:
-                add_bias(k - 2, b0, b0 + R)
+                if k == 1 and b == 0:
+                    turn_small()
+                    for later in direct[:-1]:
+                        direct_sum(later)
+            if k >= 2:
+                add_bias(k - 2, 0, blocks(k - 2))
             if k >= 1:
-                for b0 in reversed(range(0, R * len(units[k - 1]), 2 * R)):
-                    quantize(k - 1, b0, min(b0 + 2 * R, R * len(units[k - 1])))
-            if 2 <= k < joined + 2:
-                lift(k - 2)
-                join(k - 2)
-            if k < on_gpsimd and twice[k] > 0:
+                quantize(k - 1, 0, blocks(k - 1))
+            if k >= 3:
+                join(k - 3, k - 1)
+            if k in steady:
                 leaky_parts(k)
-            for b in range(early, blocks):
+            elif k >= 2:
+                lift(k - 2)
+                join(k - 2, k - 3)
+            for b in range(R, summed(k)):
                 sums(k, b)
-            if 1 <= k < closing:
-                for b0 in range(0, R * len(units[k - 1]), R):
-                    second_layer(k - 1, b0, b0 + R)
-            if k - 2 >= joined:
-                finish(k - 2, 0, R * len(units[k - 2]))
-            if k < len(units) - 1:
-                for b in range(twice[k], blocks):
-                    leaky(k, b)
+                if b == R:
+                    if k == 2:
+                        direct_sum(direct[-1])
+                    for half in range(2):
+                        if k + 2 - half in direct:
+                            direct_half(k + 2 - half, half)
+            if k in steady:
+                lift(k - 2)
+            if k >= 1:
+                second_layer(k - 1, 0, blocks(k - 1))
+            for b in range(twice[k], summed(k)):
+                leaky(k, b)
 
-        end = len(units) - 1
+        k = last - 2
+        for b in range(R):
+            sums(k, b)
+        add_bias(k - 2, 0, blocks(k - 2))
+        quantize(k - 1, 0, blocks(k - 1))
+        lift(k - 2)
+        join(k - 2, k - 1)
+        for b in range(R):
+            sums(k + 1, b)
+        second_layer(k - 1, 0, blocks(k - 1))
+        for b in range(R):
+            leaky(k, b)
+        add_bias(k - 1, 0, blocks(k - 1))
+        quantize(k, 0, R)
+        finish(k - 1, 0, blocks(k - 1))
+        for b in range(R):
+            sums(last, b)
+        second_layer(k, 0, R)
+        leaky_max(k + 1, 0, R)
+        add_bias(k, 0, R)
+        quantize(k + 1, 0, R)
+        finish(k, 0, R)
+        second_layer(k + 1, 0, R)
+
         half = R // 2
-        second_layer(end - 1, 0, R)
-        activate(end, 0, half)
-        add_bias(end - 1, 0, R)
-        quantize(end, 0, half)
-        second_layer(end, 0, half)
-        finish(end - 1, 0, R)
-        activate(end, half, R)
-        add_bias(end, 0, half)
-        quantize(end, half, R)
-        second_layer(end, half, R)
-        finish(end, 0, half)
-        add_bias(end, half, R)
-        finish(end, half, R)
+        leaky_max(last, 0, half)
+        add_bias(last - 1, 0, R)
+        quantize(last, 0, half)
+        second_layer(last, 0, half)
+        finish(last - 1, 0, R)
+        leaky_max(last, half, R)
+        add_bias(last, 0, half)
+        quantize(last, half, R)
+        second_layer(last, half, R)
+        finish(last, 0, half)
+        add_bias(last, half, R)
+        finish(last, half, R)

@@ -170,10 +170,11 @@ def tile_matchmatrix_pa_t_w4_kernel(
             x = psum.tile([P, 4, P], F32, name="x", tag="bank")
             for t in range(4):
                 nc.tensor.matmul(
-                    x[:, t, :], lhsT=a_part[h][:, t, :], rhs=picks(0), is_transpose=True, start=True, stop=False
+                    x[:, t, :], lhsT=a_part[h][:, t, :], rhs=picks(0), is_transpose=True, start=t == 0, stop=False
                 )
+            for t in range(4):
                 nc.tensor.matmul(
-                    x[:, t, :], lhsT=b_part[b % R][:, t, :], rhs=picks(s), is_transpose=True, start=False, stop=True
+                    x[:, t, :], lhsT=b_part[b % R][:, t, :], rhs=picks(s), is_transpose=True, start=False, stop=t == 3
                 )
             view = x[:].rearrange("m t c -> m c t")
             if b >= twice[k]:

@@ -148,22 +148,28 @@ def tile_matchmatrix_pa_t_w4_kernel(
         def a_rows(h, product):
             nc.vector.tensor_tensor(out=a_part[h][:], in0=product, in1=b1_all[:], op=ALU.add)
 
-        quads = [(h, s) for s in list(range(1, W)) + [0] for h in range(H)]
+        quads = [(h, s) for s in range(1, W - 1) for h in range(H)] + [(h, s) for h in (1, 0) for s in (W - 1, 0)]
         sizes = [1] + [2] * 14 + [1] * 3
         units = [list(range(sum(sizes[:k]), sum(sizes[: k + 1]))) for k in range(len(sizes))]
         most = R * max(sizes)
         last = len(units) - 1
         steady = range(2, last - 3)
-        twice = [1 if k in steady else R if k >= last - 1 else 0 for k in range(len(units))]
-        direct = range(3, last - 4, 3)
+        direct = {k: R for k in range(3, last - 3, 2)}
+        direct.update({k: 0 for k in (last - 1, last)})
+        parted = [k for k in steady if k > 2 and (k not in direct or k in (3, steady[-1]))]
+        roomy = [k for k in parted if k not in direct]
+        twice = [[0] if 2 <= k <= last - 3 else [1, 2, 3] if k >= last - 1 else [] for k in range(len(units))]
         live = [{} for k in units]
         ring = [keep.tile([P, most * P * 4], BF16, align_bytes=64, name=f"ring{i}") for i in range(RING)]
+
+        closing = [keep.tile([P, R * P * 4], BF16, align_bytes=64, name=f"closing{i}") for i in range(2)]
 
         def blocks(k):
             return R * len(units[k])
 
         def hidden(k):
-            return ring[k % RING][:].rearrange("m (b c t) -> m b c t", c=P, t=4)
+            tile = closing[last - k] if k >= last - 1 else ring[k % RING]
+            return tile[:].rearrange("m (b c t) -> m b c t", c=P, t=4)
 
         def sums(k, b):
             h, s = quads[units[k][b // R]]
@@ -177,15 +183,15 @@ def tile_matchmatrix_pa_t_w4_kernel(
                     x[:, t, :], lhsT=b_part[b % R][:, t, :], rhs=picks(s), is_transpose=True, start=False, stop=t == 3
                 )
             view = x[:].rearrange("m t c -> m c t")
-            if b >= twice[k]:
+            if b not in twice[k]:
                 first = work.tile([P, P, 4], BF16, name="first", tag="first", bufs=8)
                 nc.scalar.copy(out=first[:], in_=view)
                 live[k][b] = (view, first)
                 return
-            if b == 0:
-                live[k]["one"] = work.tile([P, twice[k], P, 4], BF16, name="one", tag="one")
-                live[k]["other"] = work.tile([P, twice[k], P, 4], BF16, name="other", tag="other")
-            if k in steady:
+            if b == twice[k][0]:
+                live[k]["one"] = work.tile([P, R, P, 4], BF16, name="one", tag="one")
+                live[k]["other"] = work.tile([P, R, P, 4], BF16, name="other", tag="other")
+            if k in parted:
                 nc.scalar.activation(out=live[k]["one"][:, b], in_=view, func=RELU)
                 nc.scalar.activation(out=live[k]["other"][:, b], in_=view, func=RELU, scale=-SLOPE)
             else:
@@ -205,13 +211,13 @@ def tile_matchmatrix_pa_t_w4_kernel(
 
         def leaky_parts(k):
             nc.gpsimd.tensor_tensor(
-                out=hidden(k)[:, : twice[k]], in0=live[k]["one"][:], in1=live[k]["other"][:], op=ALU.subtract
+                out=hidden(k)[:, 0], in0=live[k]["one"][:, 0], in1=live[k]["other"][:, 0], op=ALU.subtract
             )
 
         def quantize(k, b0, b1):
-            if b0 == 0:
-                live[k]["codes"] = work.tile([P, most * P], U32, name="codes", tag="codes", align_bytes=64)
-                live[k]["scales"] = work.tile([P, most * P], U8, name="scales", tag="scales", align_bytes=64)
+            if "codes" not in live[k]:
+                live[k]["codes"] = work.tile([P, most * P], U32, name="codes", tag="codes", align_bytes=64, bufs=3)
+                live[k]["scales"] = work.tile([P, most * P], U8, name="scales", tag="scales", align_bytes=64, bufs=3)
             cols = slice(b0 * P, b1 * P)
             nc.vector.quantize_mx(
                 out=live[k]["codes"][:, cols].bitcast(FP8X4),
@@ -236,7 +242,7 @@ def tile_matchmatrix_pa_t_w4_kernel(
                 live[k]["y", first] = y
 
         def add_bias(k, b0, b1):
-            if b0 == 0:
+            if "z" not in live[k]:
                 live[k]["z"] = work.tile([P, most, K1], F32, name="z", tag="z", bufs=3)
             for first in range(b0, b1, R):
                 n = min(R, b1 - first)
@@ -273,7 +279,7 @@ def tile_matchmatrix_pa_t_w4_kernel(
                 store(units[k][b // R], o[:, b : b + R], 0, R)
 
         def finish(k, b0, b1):
-            if b0 == 0:
+            if "o" not in live[k]:
                 live[k]["o"] = work.tile([P, blocks(k), K1], F32, name="o", tag="o", bufs=4)
             z, o = live[k]["z"], live[k]["o"]
             nc.vector.scalar_tensor_tensor(
@@ -286,41 +292,51 @@ def tile_matchmatrix_pa_t_w4_kernel(
         a_small = keep.tile([P, P, 4], F32)
         b_small = keep.tile([P, 2 * W * NB, 4], F32)
 
-        def turn_small():
-            xa = psum.tile([P, 4, P], F32, name="xa", tag="bank")
-            xb = psum.tile([P, 4, P], F32, name="xb", tag="bank")
+        def turn_small(rows):
+            bank = psum.tile([P, 4, P], F32, name="turned", tag="bank")
             for t in range(4):
-                nc.tensor.transpose(xa[:, t, :], a_part[0][:, t, :], picks(0))
-            for t in range(4):
-                nc.tensor.transpose(xb[:, t, :], b_part[R - 1][:, t, :], picks(0))
-            nc.scalar.activation(out=a_small[:], in_=xa[:].rearrange("m t c -> m c t"), func=COPY, scale=SLOPE)
-            nc.scalar.activation(
-                out=b_small[:].rearrange("m (d g) t -> m d g t", d=2),
-                in_=xb[:].rearrange("m t (g z) -> m z g t", z=Z)[:, 0].unsqueeze(1).to_broadcast([P, 2, W * NB, 4]),
-                func=COPY,
-                scale=SLOPE,
+                nc.tensor.transpose(bank[:, t, :], rows[:, t, :], picks(0))
+            return bank
+
+        def small_a():
+            nc.vector.tensor_scalar(
+                out=a_small[:], in0=turn_small(a_part[0])[:].rearrange("m t c -> m c t"), scalar1=SLOPE, scalar2=None, op0=ALU.mult
             )
 
-        def direct_sum(k):
+        def small_b():
+            once = turn_small(b_part[0])[:].rearrange("m t (g z) -> m z g t", z=Z)[:, 0]
+            nc.vector.tensor_scalar(
+                out=b_small[:].rearrange("m (d g) t -> m d g t", d=2),
+                in0=once.unsqueeze(1).to_broadcast([P, 2, W * NB, 4]),
+                scalar1=SLOPE,
+                scalar2=None,
+                op0=ALU.mult,
+            )
+
+        def direct_sum(k, after=None):
             s = quads[units[k][-1]][1]
-            low = work.tile([P, P, 4], F32, name="low", tag="low", bufs=len(direct))
+            if after is None:
+                live[k]["low"] = work.tile([P, P, 4], F32, name="low", tag="low", bufs=len(direct))
+            else:
+                live[k]["low"] = ring[after][:, : 2 * 4 * P].bitcast(F32).rearrange("m (c t) -> m c t", t=4)
             nc.gpsimd.tensor_tensor(
-                out=low[:].rearrange("m (g z) t -> m g z t", z=Z),
+                out=live[k]["low"][:].rearrange("m (g z) t -> m g z t", z=Z),
                 in0=a_small[:].rearrange("m (g z) t -> m g z t", z=Z),
                 in1=b_small[:, s * NB : (s + W) * NB, :].unsqueeze(2).to_broadcast([P, W * NB, Z, 4]),
                 op=ALU.add,
             )
-            live[k]["low"] = low
 
-        def direct_half(k, half):
-            cols = slice(half * P // 2, (half + 1) * P // 2)
-            low = live[k]["low"][:, cols]
-            high = work.tile([P, P // 2, 4], F32, name="high", tag="high")
-            nc.scalar.activation(out=high[:], in_=low, func=RELU, scale=(1.0 - SLOPE) / SLOPE)
-            nc.gpsimd.tensor_tensor(out=hidden(k)[:, blocks(k) - 1, cols], in0=low, in1=high[:], op=ALU.add)
+        def direct_relu(k):
+            live[k]["high"] = work.tile([P, P, 4], F32, name="high", tag="high", bufs=len(direct))
+            nc.scalar.activation(out=live[k]["high"][:], in_=live[k]["low"][:], func=RELU, scale=(1.0 - SLOPE) / SLOPE)
+
+        def direct_add(k, c0=0, c1=P):
+            nc.gpsimd.tensor_tensor(
+                out=hidden(k)[:, direct[k], c0:c1], in0=live[k]["low"][:, c0:c1], in1=live[k]["high"][:, c0:c1], op=ALU.add
+            )
 
         def summed(k):
-            return blocks(k) - (1 if k in direct else 0)
+            return [b for b in range(blocks(k)) if direct.get(k) != b]
 
         a_raw0 = widen(0)
         xt_a0 = turn(a_raw0[:])
@@ -355,39 +371,58 @@ def tile_matchmatrix_pa_t_w4_kernel(
         nc.scalar.copy(out=b_part[3][:], in_=pb3)
         sums(0, 0)
         a_rows(1, pa1)
+        small_a()
+        small_b()
+        direct_sum(3)
+        direct_sum(16)
 
         for k in range(last - 2):
-            for b in range(1 if k == 0 else 0, R):
+            for b in summed(k)[1 if k == 0 else 0 : R]:
                 sums(k, b)
-                if k == 1 and b == 0:
-                    turn_small()
-                    for later in direct[:-1]:
-                        direct_sum(later)
+                if k == 2 and b == 1:
+                    direct_relu(last)
             if k >= 2:
                 add_bias(k - 2, 0, blocks(k - 2))
             if k >= 1:
                 quantize(k - 1, 0, blocks(k - 1))
+            if twice[k] and k not in parted:
+                leaky_max(k, 0, 1)
+            if k == 1:
+                direct_sum(5, after=0)
+                direct_sum(last)
+                direct_sum(9)
+            if k == 2:
+                direct_sum(7, after=1)
+                direct_sum(11)
+                direct_sum(13)
             if k >= 3:
                 join(k - 3, k - 1)
-            if k in steady:
+            if k in parted:
                 leaky_parts(k)
-            elif k >= 2:
+            if k == last - 3:
                 lift(k - 2)
                 join(k - 2, k - 3)
-            for b in range(R, summed(k)):
+            if k in direct and k + 2 in steady:
+                direct_add(k + 2)
+            for b in summed(k)[R:]:
                 sums(k, b)
-                if b == R:
-                    if k == 2:
-                        direct_sum(direct[-1])
-                    for half in range(2):
-                        if k + 2 - half in direct:
-                            direct_half(k + 2 - half, half)
+                if k == 1 and b == R:
+                    direct_relu(3)
+                    direct_add(3)
+                if k == 1 and b == R + 2:
+                    direct_relu(last - 1)
+                if k in roomy[:4] and b == R + 1:
+                    closer, half = divmod(roomy.index(k), 2)
+                    direct_add(last - 1 + closer, half * P // 2, (half + 1) * P // 2)
             if k in steady:
                 lift(k - 2)
+            if k >= 2 and k + 3 in direct and k + 3 in steady:
+                direct_relu(k + 3)
             if k >= 1:
                 second_layer(k - 1, 0, blocks(k - 1))
-            for b in range(twice[k], summed(k)):
-                leaky(k, b)
+            for b in summed(k):
+                if b not in twice[k]:
+                    leaky(k, b)
 
         k = last - 2
         for b in range(R):
@@ -396,7 +431,7 @@ def tile_matchmatrix_pa_t_w4_kernel(
         quantize(k - 1, 0, blocks(k - 1))
         lift(k - 2)
         join(k - 2, k - 1)
-        for b in range(R):
+        for b in summed(k + 1):
             sums(k + 1, b)
         second_layer(k - 1, 0, blocks(k - 1))
         for b in range(R):
@@ -404,25 +439,22 @@ def tile_matchmatrix_pa_t_w4_kernel(
         add_bias(k - 1, 0, blocks(k - 1))
         quantize(k, 0, R)
         finish(k - 1, 0, blocks(k - 1))
-        for b in range(R):
+        for b in summed(last):
             sums(last, b)
         second_layer(k, 0, R)
-        leaky_max(k + 1, 0, R)
+        leaky_max(k + 1, 1, R)
         add_bias(k, 0, R)
         quantize(k + 1, 0, R)
-        finish(k, 0, R)
         second_layer(k + 1, 0, R)
-
-        half = R // 2
-        leaky_max(last, 0, half)
-        add_bias(last - 1, 0, R)
-        quantize(last, 0, half)
-        second_layer(last, 0, half)
-        finish(last - 1, 0, R)
-        leaky_max(last, half, R)
-        add_bias(last, 0, half)
-        quantize(last, half, R)
-        second_layer(last, half, R)
-        finish(last, 0, half)
-        add_bias(last, half, R)
-        finish(last, half, R)
+        finish(k, 0, R)
+        leaky_max(last, 1, R)
+        add_bias(k + 1, 0, R)
+        halves = ((0, R // 2), (R // 2, R))
+        for b0, b1 in halves:
+            quantize(last, b0, b1)
+            second_layer(last, b0, b1)
+        finish(k + 1, 0, R)
+        for b0, b1 in halves:
+            add_bias(last, b0, b1)
+        for b0, b1 in halves:
+            finish(last, b0, b1)

@@ -154,11 +154,11 @@ def tile_matchmatrix_pa_t_w4_kernel(
         most = R * max(sizes)
         last = len(units) - 1
         steady = range(2, last - 3)
-        direct = {k: R for k in range(3, last - 3, 2)}
+        middle = range(3, last - 4, 3)
+        direct = {k: R for k in middle}
         direct.update({k: 0 for k in (last - 1, last)})
-        parted = [k for k in steady if k > 2 and (k not in direct or k in (3, steady[-1]))]
-        roomy = [k for k in parted if k not in direct]
-        twice = [[0] if 2 <= k <= last - 3 else [1, 2, 3] if k >= last - 1 else [] for k in range(len(units))]
+        parted = steady[1:]
+        twice = [[0] if 2 <= k <= last - 2 else [1, 2, 3] if k >= last - 1 else [] for k in range(len(units))]
         live = [{} for k in units]
         ring = [keep.tile([P, most * P * 4], BF16, align_bytes=64, name=f"ring{i}") for i in range(RING)]
 
@@ -373,14 +373,14 @@ def tile_matchmatrix_pa_t_w4_kernel(
         a_rows(1, pa1)
         small_a()
         small_b()
-        direct_sum(3)
-        direct_sum(16)
+        direct_sum(middle[0])
+        direct_sum(last - 1)
 
         for k in range(last - 2):
             for b in summed(k)[1 if k == 0 else 0 : R]:
                 sums(k, b)
-                if k == 2 and b == 1:
-                    direct_relu(last)
+                if k == 1 and b < 2:
+                    direct_relu((middle[0], last - 1)[b])
             if k >= 2:
                 add_bias(k - 2, 0, blocks(k - 2))
             if k >= 1:
@@ -388,36 +388,34 @@ def tile_matchmatrix_pa_t_w4_kernel(
             if twice[k] and k not in parted:
                 leaky_max(k, 0, 1)
             if k == 1:
-                direct_sum(5, after=0)
-                direct_sum(last)
-                direct_sum(9)
+                direct_sum(middle[1], after=0)
+                direct_sum(middle[3])
+                direct_add(middle[0])
+                direct_add(last - 1)
             if k == 2:
-                direct_sum(7, after=1)
-                direct_sum(11)
-                direct_sum(13)
+                direct_sum(last, after=1)
+                direct_sum(middle[2])
             if k >= 3:
                 join(k - 3, k - 1)
             if k in parted:
                 leaky_parts(k)
+            if k == 3:
+                direct_add(last)
             if k == last - 3:
                 lift(k - 2)
                 join(k - 2, k - 3)
-            if k in direct and k + 2 in steady:
-                direct_add(k + 2)
             for b in summed(k)[R:]:
                 sums(k, b)
-                if k == 1 and b == R:
-                    direct_relu(3)
-                    direct_add(3)
-                if k == 1 and b == R + 2:
-                    direct_relu(last - 1)
-                if k in roomy[:4] and b == R + 1:
-                    closer, half = divmod(roomy.index(k), 2)
-                    direct_add(last - 1 + closer, half * P // 2, (half + 1) * P // 2)
+                if b == R + 1:
+                    for half in range(2):
+                        if k + 2 - half in middle[1:]:
+                            direct_add(k + 2 - half, half * P // 2, (half + 1) * P // 2)
+            if k == 2:
+                direct_relu(last)
+            if k + 3 in middle[1:]:
+                direct_relu(k + 3)
             if k in steady:
                 lift(k - 2)
-            if k >= 2 and k + 3 in direct and k + 3 in steady:
-                direct_relu(k + 3)
             if k >= 1:
                 second_layer(k - 1, 0, blocks(k - 1))
             for b in summed(k):
@@ -429,12 +427,13 @@ def tile_matchmatrix_pa_t_w4_kernel(
             sums(k, b)
         add_bias(k - 2, 0, blocks(k - 2))
         quantize(k - 1, 0, blocks(k - 1))
+        leaky_max(k, 0, 1)
         lift(k - 2)
         join(k - 2, k - 1)
         for b in summed(k + 1):
             sums(k + 1, b)
         second_layer(k - 1, 0, blocks(k - 1))
-        for b in range(R):
+        for b in range(1, R):
             leaky(k, b)
         add_bias(k - 1, 0, blocks(k - 1))
         quantize(k, 0, R)

@@ -148,7 +148,8 @@ def tile_matchmatrix_pa_t_w4_kernel(
         def a_rows(h, product):
             nc.vector.tensor_tensor(out=a_part[h][:], in0=product, in1=b1_all[:], op=ALU.add)
 
-        quads = [(h, s) for s in range(1, W - 1) for h in range(H)] + [(h, s) for h in (1, 0) for s in (W - 1, 0)]
+        order = sorted(range(W), key=lambda s: -min(s, W - s))
+        quads = [(h, s) for s in order[:-2] for h in range(H)] + [(h, s) for s in order[-2:] for h in (1, 0)]
         sizes = [1] + [2] * 14 + [1] * 3
         units = [list(range(sum(sizes[:k]), sum(sizes[: k + 1]))) for k in range(len(sizes))]
         most = R * max(sizes)
@@ -156,9 +157,10 @@ def tile_matchmatrix_pa_t_w4_kernel(
         steady = range(2, last - 3)
         middle = range(3, last - 4, 3)
         direct = {k: R for k in middle}
-        direct.update({k: 0 for k in (last - 1, last)})
+        closers = (last - 2, last)
+        direct.update({k: 0 for k in closers})
         parted = steady[1:]
-        twice = [[0] if 2 <= k <= last - 2 else [1, 2, 3] if k >= last - 1 else [] for k in range(len(units))]
+        twice = [[0] if 2 <= k <= last - 3 else [] for k in range(last - 2)] + [[], [1, 2, 3], [1, 2, 3]]
         live = [{} for k in units]
         ring = [keep.tile([P, most * P * 4], BF16, align_bytes=64, name=f"ring{i}") for i in range(RING)]
 
@@ -168,7 +170,7 @@ def tile_matchmatrix_pa_t_w4_kernel(
             return R * len(units[k])
 
         def hidden(k):
-            tile = closing[last - k] if k >= last - 1 else ring[k % RING]
+            tile = closing[closers.index(k)] if k in closers else ring[k % RING]
             return tile[:].rearrange("m (b c t) -> m b c t", c=P, t=4)
 
         def sums(k, b):
@@ -374,13 +376,13 @@ def tile_matchmatrix_pa_t_w4_kernel(
         small_a()
         small_b()
         direct_sum(middle[0])
-        direct_sum(last - 1)
+        direct_sum(closers[0])
 
         for k in range(last - 2):
             for b in summed(k)[1 if k == 0 else 0 : R]:
                 sums(k, b)
                 if k == 1 and b < 2:
-                    direct_relu((middle[0], last - 1)[b])
+                    direct_relu((middle[0], closers[0])[b])
             if k >= 2:
                 add_bias(k - 2, 0, blocks(k - 2))
             if k >= 1:
@@ -391,7 +393,7 @@ def tile_matchmatrix_pa_t_w4_kernel(
                 direct_sum(middle[1], after=0)
                 direct_sum(middle[3])
                 direct_add(middle[0])
-                direct_add(last - 1)
+                direct_add(closers[0])
             if k == 2:
                 direct_sum(last, after=1)
                 direct_sum(middle[2])
@@ -423,18 +425,18 @@ def tile_matchmatrix_pa_t_w4_kernel(
                     leaky(k, b)
 
         k = last - 2
-        for b in range(R):
+        for b in summed(k):
             sums(k, b)
         add_bias(k - 2, 0, blocks(k - 2))
         quantize(k - 1, 0, blocks(k - 1))
-        leaky_max(k, 0, 1)
         lift(k - 2)
         join(k - 2, k - 1)
         for b in summed(k + 1):
             sums(k + 1, b)
         second_layer(k - 1, 0, blocks(k - 1))
-        for b in range(1, R):
+        for b in summed(k):
             leaky(k, b)
+        leaky(k + 1, 0)
         add_bias(k - 1, 0, blocks(k - 1))
         quantize(k, 0, R)
         finish(k - 1, 0, blocks(k - 1))

from contextlib import ExitStack

import concourse.mybir as mybir
from concourse.masks import make_identity

F32 = mybir.dt.float32
BF16 = mybir.dt.bfloat16
I32 = mybir.dt.int32
U32 = mybir.dt.uint32
U8 = mybir.dt.uint8
FP8 = mybir.dt.float8_e4m3fn
FP8X4 = mybir.dt.float8_e4m3fn_x4
FP4X4 = mybir.dt.float4_e2m1fn_x4
ALU = mybir.AluOpType
COPY = mybir.ActivationFunctionType.Copy
RELU = mybir.ActivationFunctionType.Relu

P = 128
NB, NI, NJ, D, K0, K1 = 2, 128, 64, 512, 512, 128
FLOPS = 2 * (NB * (NI + NJ) * D * K0 + NB * NI * NJ * K0 * K1)
SLOPE = 0.01
R = 4
W = NJ // R
Z = P // (NB * W)
M = NB * Z
H = NB * NI // P
RING = 6


def tile_matchmatrix_pa_t_w4_kernel(
    tc, sent_a_bytes, sent_a_scale, sent_b, w1_words, w1_scales, b1, w2_words, w2_scales, b2, out
):
    nc = tc.nc
    with ExitStack() as ctx:
        keep = ctx.enter_context(tc.tile_pool(name="keep", bufs=1))
        work = ctx.enter_context(tc.tile_pool(name="work", bufs=2))
        psum = ctx.enter_context(tc.psum_pool(name="psum", bufs=8))
        ctx.enter_context(tc.manual_schedule())

        b_raw = keep.tile([P, D], BF16, align_bytes=64)
        a_bytes = keep.tile([P, H * D], U8, align_bytes=64)
        a_scale = keep.tile([P, 4], F32)
        b1_cols = keep.tile([P, 4], BF16)
        b1_all = keep.tile([P, 4, P], F32)
        b2_all = keep.tile([P, K1], BF16)
        w1 = keep.tile([P, 2, 2 * K0], U8, align_bytes=64)
        w1_sc = keep.tile([P, 2, K0], U8, align_bytes=64)
        w2 = keep.tile([P, 2 * K1], U8, align_bytes=64)
        w2_sc = keep.tile([P, K1], U8, align_bytes=64)
        nc.vector.memset(w1_sc[:].rearrange("p g n -> p (g n)").bitcast(I32), 0)
        nc.vector.memset(w2_sc[:].bitcast(I32), 0)
        nc.sync.dma_start(out=a_bytes[:], in_=sent_a_bytes.rearrange("n (x h) k -> (n x) (h k)", h=H))
        nc.sync.dma_start(out=b_raw[:], in_=sent_b.rearrange("n j k -> (n j) k"))
        nc.sync.dma_start(out=a_scale[:], in_=sent_a_scale.rearrange("x y (p t) -> p (x y t)", t=4))
        for q in range(4):
            nc.sync.dma_start(
                out=w1_sc[32 * q : 32 * q + 4, :, :].bitcast(I32),
                in_=w1_scales[:, 4 * q : 4 * q + 4, :].rearrange("g q n -> q g n").bitcast(I32),
            )
        nc.sync.dma_start(out=w1[:].bitcast(I32), in_=w1_words.rearrange("g p n -> p g n").bitcast(I32))
        nc.sync.dma_start(out=b1_cols[:], in_=b1.rearrange("(m t) -> m t", t=4))
        nc.sync.dma_start(out=w2[:].bitcast(I32), in_=w2_words[0].bitcast(I32))
        for q in range(4):
            nc.sync.dma_start(
                out=w2_sc[32 * q : 32 * q + 4, :].bitcast(I32),
                in_=w2_scales[0, 4 * q : 4 * q + 4, :].bitcast(I32),
            )
        nc.sync.dma_start(out=b2_all[:], in_=b2.partition_broadcast(P))

        ident = keep.tile([P, P], F32)
        make_identity(nc, ident[:])
        shifts = keep.tile([P, 2 * W, M], F32)
        for half in range(2):
            nc.vector.tensor_copy(
                out=shifts[:, half * W : (half + 1) * W, :], in_=ident[:].rearrange("q (m w) -> q w m", w=W)
            )
        ident_bf = keep.tile([P, P], BF16)
        nc.vector.tensor_copy(out=ident_bf[:], in_=ident[:])

        def picks(s):
            return shifts[:].rearrange("q w m -> q (w m)")[:, s * M : s * M + P]

        def turn(raw):
            words = raw.bitcast(F32)
            xt = psum.tile([P, 2, P], F32, name="xt", tag="bank")
            for u in range(2):
                nc.tensor.transpose(xt[:, u, :], words[:, u : 2 * P : 2], ident[:])
            return xt

        b_grouped = keep.tile([P, R * P * 4], BF16, align_bytes=64)
        b_codes = keep.tile([P, R * P], U32, align_bytes=64)
        b_scales = keep.tile([P, R * P], U8, align_bytes=64)
        a_part = [keep.tile([P, 4, P], F32, name=f"a_part{h}") for h in range(H)]
        b_part = [keep.tile([P, 4, P], F32, name=f"b_part{r}") for r in range(R)]

        def widen(h):
            a_raw = keep.tile([P, D], BF16, align_bytes=64, name=f"a_raw{h}")
            nc.vector.tensor_copy(out=a_raw[:], in_=a_bytes[:, h * D : (h + 1) * D].bitcast(FP8))
            return a_raw

        def group_b(xt, r):
            nc.scalar.copy(
                out=b_grouped[:, r * D : (r + 1) * D].bitcast(F32).rearrange("p (n z w u) -> p n z w u", n=NB, z=Z, u=2),
                in_=xt[:].rearrange("p u (n w r) -> p r n w u", n=NB, r=R)[:, r].unsqueeze(2).to_broadcast([P, NB, Z, W, 2]),
            )

        def quantize_b(r0, r1):
            nc.vector.quantize_mx(
                out=b_codes[:, r0 * P : r1 * P].bitcast(FP8X4),
                scales=b_scales[:, r0 * P : r1 * P],
                in_=b_grouped[:, r0 * D : r1 * D],
            )

        def scale_a(h, xt):
            a_grouped = keep.tile([P, P, 2, 2], BF16, align_bytes=64, name=f"a_grouped{h}")
            nc.vector.tensor_tensor(
                out=a_grouped[:],
                in0=xt[:].rearrange("p u c -> p (u c)").bitcast(BF16).rearrange("p (u c e) -> p c u e", u=2, e=2),
                in1=a_scale[:].rearrange("p (u e) -> p u e", u=2).unsqueeze(1).to_broadcast([P, P, 2, 2]),
                op=ALU.mult,
            )
            return a_grouped

        def quantize_a(h, a_grouped):
            a_codes = keep.tile([P, P], U32, align_bytes=64, name=f"a_codes{h}")
            a_scales = keep.tile([P, P], U8, align_bytes=64, name=f"a_scales{h}")
            nc.vector.quantize_mx(
                out=a_codes[:].bitcast(FP8X4), scales=a_scales[:], in_=a_grouped[:].rearrange("p c u e -> p (c u e)")
            )
            return a_codes[:], a_scales[:]

        def first_layer(codes, scales, g):
            bank = psum.tile([P, K0], F32, name="product", tag="bank")
            nc.tensor.matmul_mx(
                out=bank[:],
                lhsT=codes.bitcast(FP8X4),
                lhsT_scale=scales,
                rhs=w1[:, g, :].bitcast(FP4X4),
                rhs_scale=w1_sc[:, g, :],
                start=True,
                stop=True,
            )
            return bank[:].rearrange("q (m t) -> q t m", t=4)

        def b_product(r):
            return first_layer(b_codes[:, r * P : (r + 1) * P], b_scales[:, r * P : (r + 1) * P], 1)

        def a_rows(h, product):
            nc.vector.tensor_tensor(out=a_part[h][:], in0=product, in1=b1_all[:], op=ALU.add)

        order = sorted(range(W), key=lambda s: -min(s, W - s))
        quads = [(h, s) for s in order[:-2] for h in range(H)] + [(h, s) for s in order[-2:] for h in (1, 0)]
        sizes = [1] + [2] * 14 + [1] * 3
        units = [list(range(sum(sizes[:k]), sum(sizes[: k + 1]))) for k in range(len(sizes))]
        most = R * max(sizes)
        last = len(units) - 1
        steady = range(2, last - 3)
        middle = range(3, last - 4, 3)
        direct = {k: R for k in middle}
        closers = (last - 2, last)
        direct.update({k: 0 for k in closers})
        parted = steady[1:]
        twice = [[0] if 2 <= k <= last - 3 else [] for k in range(last - 2)] + [[], [1, 2, 3], [1, 2, 3]]
        live = [{} for k in units]
        ring = [keep.tile([P, most * P * 4], BF16, align_bytes=64, name=f"ring{i}") for i in range(RING)]

        closing = [keep.tile([P, R * P * 4], BF16, align_bytes=64, name=f"closing{i}") for i in range(2)]

        def blocks(k):
            return R * len(units[k])

        def hidden(k):
            tile = closing[closers.index(k)] if k in closers else ring[k % RING]
            return tile[:].rearrange("m (b c t) -> m b c t", c=P, t=4)

        def sums(k, b):
            h, s = quads[units[k][b // R]]
            x = psum.tile([P, 4, P], F32, name="x", tag="bank")
            for t in range(4):
                nc.tensor.matmul(
                    x[:, t, :], lhsT=a_part[h][:, t, :], rhs=picks(0), is_transpose=True, start=t == 0, stop=False
                )
            for t in range(4):
                nc.tensor.matmul(
                    x[:, t, :], lhsT=b_part[b % R][:, t, :], rhs=picks(s), is_transpose=True, start=False, stop=t == 3
                )
            view = x[:].rearrange("m t c -> m c t")
            if b not in twice[k]:
                first = work.tile([P, P, 4], BF16, name="first", tag="first", bufs=8)
                nc.scalar.copy(out=first[:], in_=view)
                live[k][b] = (view, first)
                return
            if b == twice[k][0]:
                live[k]["one"] = work.tile([P, R, P, 4], BF16, name="one", tag="one")
                live[k]["other"] = work.tile([P, R, P, 4], BF16, name="other", tag="other")
            if k in parted:
                nc.scalar.activation(out=live[k]["one"][:, b], in_=view, func=RELU)
                nc.scalar.activation(out=live[k]["other"][:, b], in_=view, func=RELU, scale=-SLOPE)
            else:
                nc.scalar.copy(out=live[k]["one"][:, b], in_=view)
                nc.scalar.activation(out=live[k]["other"][:, b], in_=view, func=COPY, scale=SLOPE)

        def leaky(k, b):
            view, first = live[k][b]
            nc.vector.scalar_tensor_tensor(
                out=hidden(k)[:, b], in0=view, scalar=SLOPE, in1=first[:], op0=ALU.mult, op1=ALU.max
            )

        def leaky_max(k, b0, b1):
            nc.vector.tensor_tensor(
                out=hidden(k)[:, b0:b1], in0=live[k]["one"][:, b0:b1], in1=live[k]["other"][:, b0:b1], op=ALU.max
            )

        def leaky_parts(k):
            nc.gpsimd.tensor_tensor(
                out=hidden(k)[:, 0], in0=live[k]["one"][:, 0], in1=live[k]["other"][:, 0], op=ALU.subtract
            )

        def quantize(k, b0, b1):
            if "codes" not in live[k]:
                live[k]["codes"] = work.tile([P, most * P], U32, name="codes", tag="codes", align_bytes=64, bufs=3)
                live[k]["scales"] = work.tile([P, most * P], U8, name="scales", tag="scales", align_bytes=64, bufs=3)
            cols = slice(b0 * P, b1 * P)
            nc.vector.quantize_mx(
                out=live[k]["codes"][:, cols].bitcast(FP8X4),
                scales=live[k]["scales"][:, cols],
                in_=hidden(k)[:, b0:b1].rearrange("m b c t -> m (b c t)"),
            )

        def second_layer(k, b0, b1):
            for first in range(b0, b1, R):
                y = psum.tile([P, R, K1], F32, name="y", tag="bank")
                for b in range(first, min(first + R, b1)):
                    cols = slice(b * P, (b + 1) * P)
                    nc.tensor.matmul_mx(
                        out=y[:, b - first, :],
                        lhsT=live[k]["codes"][:, cols].bitcast(FP8X4),
                        lhsT_scale=live[k]["scales"][:, cols],
                        rhs=w2[:].bitcast(FP4X4),
                        rhs_scale=w2_sc[:],
                        start=True,
                        stop=True,
                    )
                live[k]["y", first] = y

        def add_bias(k, b0, b1):
            if "z" not in live[k]:
                live[k]["z"] = work.tile([P, most, K1], F32, name="z", tag="z", bufs=3)
            for first in range(b0, b1, R):
                n = min(R, b1 - first)
                nc.vector.tensor_tensor(
                    out=live[k]["z"][:, first : first + n],
                    in0=live[k]["y", first][:, :n],
                    in1=b2_all[:].unsqueeze(1).to_broadcast([P, n, K1]),
                    op=ALU.add,
                )

        runs = out.rearrange("n (z x) (g r) k -> (n z) (x g) (r k)", z=Z, r=R)
        step = H * W + 1

        def store(q, o, r0, r1):
            h, s = quads[q]
            for w0, w1 in ((0, W - s), (W - s, W)) if s else ((0, W),):
                start = w0 * step + h * W + (w0 + s) % W - w0
                nc.sync.dma_start(
                    out=runs[:, start : start + (w1 - w0 - 1) * step + 1 : step, r0 * K1 : r1 * K1].rearrange("m w x -> w m x"),
                    in_=o[w0 * M : w1 * M].rearrange("c r k -> c (r k)"),
                )

        def lift(k):
            live[k]["lift"] = work.tile([P, most, K1], F32, name="lift", tag="lift")
            nc.scalar.activation(
                out=live[k]["lift"][:, : blocks(k)], in_=live[k]["z"][:, : blocks(k)], func=RELU, scale=SLOPE - 1.0
            )

        def join(k, after):
            o = ring[after % RING][:].bitcast(F32).rearrange("c (b k) -> c b k", k=K1)
            n = blocks(k)
            nc.gpsimd.tensor_tensor(out=o[:, :n], in0=live[k]["z"][:, :n], in1=live[k]["lift"][:, :n], op=ALU.add)
            for b in range(0, n, R):
                store(units[k][b // R], o[:, b : b + R], 0, R)

        def finish(k, b0, b1):
            if "o" not in live[k]:
                live[k]["o"] = work.tile([P, blocks(k), K1], F32, name="o", tag="o", bufs=4)
            z, o = live[k]["z"], live[k]["o"]
            nc.vector.scalar_tensor_tensor(
                out=o[:, b0:b1], in0=z[:, b0:b1], scalar=SLOPE, in1=z[:, b0:b1], op0=ALU.mult, op1=ALU.max
            )
            for b in range(b0, b1, R):
                end = min(b + R, b1)
                store(units[k][b // R], o[:, b:end], b % R, b % R + end - b)

        a_small = keep.tile([P, P, 4], F32)
        b_small = keep.tile([P, 2 * W * NB, 4], F32)

        def turn_small(rows):
            bank = psum.tile([P, 4, P], F32, name="turned", tag="bank")
            for t in range(4):
                nc.tensor.transpose(bank[:, t, :], rows[:, t, :], picks(0))
            return bank

        def small_a():
            nc.vector.tensor_scalar(
                out=a_small[:], in0=turn_small(a_part[0])[:].rearrange("m t c -> m c t"), scalar1=SLOPE, scalar2=None, op0=ALU.mult
            )

        def small_b():
            once = turn_small(b_part[0])[:].rearrange("m t (g z) -> m z g t", z=Z)[:, 0]
            nc.vector.tensor_scalar(
                out=b_small[:].rearrange("m (d g) t -> m d g t", d=2),
                in0=once.unsqueeze(1).to_broadcast([P, 2, W * NB, 4]),
                scalar1=SLOPE,
                scalar2=None,
                op0=ALU.mult,
            )

        def direct_sum(k, after=None):
            s = quads[units[k][-1]][1]
            if after is None:
                live[k]["low"] = work.tile([P, P, 4], F32, name="low", tag="low", bufs=len(direct))
            else:
                live[k]["low"] = ring[after][:, : 2 * 4 * P].bitcast(F32).rearrange("m (c t) -> m c t", t=4)
            nc.gpsimd.tensor_tensor(
                out=live[k]["low"][:].rearrange("m (g z) t -> m g z t", z=Z),
                in0=a_small[:].rearrange("m (g z) t -> m g z t", z=Z),
                in1=b_small[:, s * NB : (s + W) * NB, :].unsqueeze(2).to_broadcast([P, W * NB, Z, 4]),
                op=ALU.add,
            )

        def direct_relu(k):
            live[k]["high"] = work.tile([P, P, 4], F32, name="high", tag="high", bufs=len(direct))
            nc.scalar.activation(out=live[k]["high"][:], in_=live[k]["low"][:], func=RELU, scale=(1.0 - SLOPE) / SLOPE)

        def direct_add(k, c0=0, c1=P):
            nc.gpsimd.tensor_tensor(
                out=hidden(k)[:, direct[k], c0:c1], in0=live[k]["low"][:, c0:c1], in1=live[k]["high"][:, c0:c1], op=ALU.add
            )

        def summed(k):
            return [b for b in range(blocks(k)) if direct.get(k) != b]

        a_raw0 = widen(0)
        xt_a0 = turn(a_raw0[:])
        xt_b = turn(b_raw[:])
        a_raw1 = widen(1)
        xt_a1 = turn(a_raw1[:])
        spread = psum.tile([P, 4, P], F32, name="spread", tag="bank")
        for t in range(4):
            nc.tensor.matmul(
                spread[:, t, :], lhsT=b1_cols[:, t : t + 1].to_broadcast([P, P]), rhs=ident_bf[:], start=True, stop=True
            )
        grouped0 = scale_a(0, xt_a0)
        for r in range(R):
            group_b(xt_b, r)
        nc.scalar.copy(out=b1_all[:], in_=spread[:])
        quantized0 = quantize_a(0, grouped0)
        quantize_b(0, 1)
        quantize_b(1, 2)
        grouped1 = scale_a(1, xt_a1)
        pa0 = first_layer(*quantized0, 0)
        pb0 = b_product(0)
        pb1 = b_product(1)
        nc.scalar.copy(out=b_part[0][:], in_=pb0)
        quantize_b(2, R)
        quantized1 = quantize_a(1, grouped1)
        a_rows(0, pa0)
        pb2 = b_product(2)
        pb3 = b_product(3)
        nc.scalar.copy(out=b_part[1][:], in_=pb1)
        nc.vector.tensor_copy(out=b_part[2][:], in_=pb2)
        pa1 = first_layer(*quantized1, 0)
        nc.scalar.copy(out=b_part[3][:], in_=pb3)
        sums(0, 0)
        a_rows(1, pa1)
        small_a()
        small_b()
        direct_sum(middle[0])
        direct_sum(closers[0])

        for k in range(last - 2):
            for b in summed(k)[1 if k == 0 else 0 : R]:
                sums(k, b)
                if k == 1 and b < 2:
                    direct_relu((middle[0], closers[0])[b])
            if k >= 2:
                add_bias(k - 2, 0, blocks(k - 2))
            if k >= 1:
                quantize(k - 1, 0, blocks(k - 1))
            if twice[k] and k not in parted:
                leaky_max(k, 0, 1)
            if k == 1:
                direct_sum(middle[1], after=0)
                direct_sum(middle[3])
                direct_add(middle[0])
                direct_add(closers[0])
            if k == 2:
                direct_sum(last, after=1)
                direct_sum(middle[2])
            if k >= 3:
                join(k - 3, k - 1)
            if k in parted:
                leaky_parts(k)
            if k == 3:
                direct_add(last)
            if k == last - 3:
                lift(k - 2)
                join(k - 2, k - 3)
            for b in summed(k)[R:]:
                sums(k, b)
                if b == R + 1:
                    for half in range(2):
                        if k + 2 - half in middle[1:]:
                            direct_add(k + 2 - half, half * P // 2, (half + 1) * P // 2)
            if k == 2:
                direct_relu(last)
            if k + 3 in middle[1:]:
                direct_relu(k + 3)
            if k in steady:
                lift(k - 2)
            if k >= 1:
                second_layer(k - 1, 0, blocks(k - 1))
            for b in summed(k):
                if b not in twice[k]:
                    leaky(k, b)

        k = last - 2
        for b in summed(k):
            sums(k, b)
        add_bias(k - 2, 0, blocks(k - 2))
        quantize(k - 1, 0, blocks(k - 1))
        lift(k - 2)
        join(k - 2, k - 1)
        for b in summed(k + 1):
            sums(k + 1, b)
        second_layer(k - 1, 0, blocks(k - 1))
        for b in summed(k):
            leaky(k, b)
        leaky(k + 1, 0)
        add_bias(k - 1, 0, blocks(k - 1))
        quantize(k, 0, R)
        finish(k - 1, 0, blocks(k - 1))
        for b in summed(last):
            sums(last, b)
        second_layer(k, 0, R)
        leaky_max(k + 1, 1, R)
        add_bias(k, 0, R)
        quantize(k + 1, 0, R)
        second_layer(k + 1, 0, R)
        finish(k, 0, R)
        leaky_max(last, 1, R)
        add_bias(k + 1, 0, R)
        halves = ((0, R // 2), (R // 2, R))
        for b0, b1 in halves:
            quantize(last, b0, b1)
            second_layer(last, b0, b1)
        finish(k + 1, 0, R)
        for b0, b1 in halves:
            add_bias(last, b0, b1)
        for b0, b1 in halves:
            finish(last, b0, b1)
